import numpy as np
import ml_dtypes


def mxq(x, axis, fmt="e4m3"):
    dtype, down = {"e4m3": (ml_dtypes.float8_e4m3fn, 7), "e5m2": (ml_dtypes.float8_e5m2, 14)}[fmt]
    v = np.moveaxis(np.asarray(x, np.float32).astype(ml_dtypes.bfloat16).astype(np.float64), axis, -1)
    blocks = v.reshape(v.shape[:-1] + (-1, 32))
    amax = np.abs(blocks).max(-1, keepdims=True)
    byte = np.maximum(np.where(amax > 0, np.frexp(amax)[1] - 1 + 127, 0) - down, 1)
    scale = np.exp2(byte - 127.0)
    codes = (blocks / scale).astype(np.float32).astype(dtype).astype(np.float64)
    return np.moveaxis((codes * scale).reshape(v.shape), -1, axis)


WIDE = False


def mx_kscale(k):
    if not WIDE:
        return np.ones(k)
    levels = np.array([10, -10, 5, -5, 0])
    a = np.random.permutation(np.resize(levels, k // 512 * 4)).reshape(k // 512, 4)
    idx = np.arange(k)
    return np.exp2(a[idx // 512, idx % 128 // 32])


BF16 = ml_dtypes.bfloat16


def bf(x):
    return np.asarray(x, np.float32).astype(BF16)


def f64(x):
    return np.asarray(x).astype(np.float64)


E2M1 = np.array([0.0, 0.5, 1.0, 1.5, 2.0, 3.0, 4.0, 6.0, -0.0, -0.5, -1.0, -1.5, -2.0, -3.0, -4.0, -6.0])


def pack_weight(w, fmt):
    k, n = w.shape
    w = f64(bf(w)).reshape(k // 32, 32, n)
    amax = np.abs(w).max(1)
    if fmt == "e4m3":
        byte = np.frexp(amax)[1] - 1 + 127 - 7
    else:
        mant, ex = np.frexp(amax / 6.0)
        byte = np.where(mant > 0.5, ex, ex - 1) + 127
    byte = np.clip(np.where(amax > 0, byte, 1), 1, 254)
    scaled = (w * np.exp2(127.0 - byte)[:, None, :]).reshape(k, n).astype(np.float32)
    by_word = np.ascontiguousarray(scaled.reshape(k // 512, 128, 4, n).transpose(0, 1, 3, 2))
    if fmt == "e4m3":
        words = by_word.astype(ml_dtypes.float8_e4m3fn).view(np.uint8)
    else:
        c = by_word.astype(ml_dtypes.float4_e2m1fn).view(np.uint8) & 0xF
        words = c[..., 0::2] | (c[..., 1::2] << 4)
    return np.ascontiguousarray(words), np.ascontiguousarray(byte.astype(np.uint8).reshape(k // 512, 16, n))


def unpack_weight(words, scales, fmt):
    g, p, n, _ = words.shape
    if fmt == "e4m3":
        vals = np.ascontiguousarray(words).view(ml_dtypes.float8_e4m3fn).astype(np.float64)
    else:
        nib = np.empty((g, p, n, 4), np.uint8)
        nib[..., 0::2] = words & 0xF
        nib[..., 1::2] = words >> 4
        vals = E2M1[nib]
    vals = vals * np.repeat(np.exp2(scales.astype(np.float64) - 127.0), 8, axis=1)[..., None]
    return vals.transpose(0, 1, 3, 2).reshape(g * 512, n)


B, L, D, H, DK = 16, 256, 512, 4, 64
E = H * DK
FMT = "e4m3"


def tropical_linear(t, w):
    return np.stack([np.max(t[n][:, None, :] + w[None, :, :], axis=-1) for n in range(t.shape[0])])


def split_heads(t):
    return t.reshape(B, L, H, DK).transpose(0, 2, 1, 3).reshape(B * H, L, DK)


def proj(xq, words, scales, lam):
    return np.log1p(np.maximum(xq @ unpack_weight(words, scales, FMT), 0.0)) - lam


def setup_inputs():
    s = mx_kscale(D)
    x = bf(np.random.standard_normal((B, L, D)) * s)
    Wq_words, Wq_scales = pack_weight(np.ascontiguousarray((np.random.standard_normal((E, D)) / np.sqrt(D) / s[None, :]).T), FMT)
    Wk_words, Wk_scales = pack_weight(np.ascontiguousarray((np.random.standard_normal((E, D)) / np.sqrt(D) / s[None, :]).T), FMT)
    Wv_words, Wv_scales = pack_weight(np.ascontiguousarray((np.random.standard_normal((E, D)) / np.sqrt(D) / s[None, :]).T), FMT)
    return {"x": x,
            "Wq_words": Wq_words, "Wq_scales": Wq_scales,
            "Wk_words": Wk_words, "Wk_scales": Wk_scales,
            "Wv_words": Wv_words, "Wv_scales": Wv_scales,
            "lam": bf(1.0 + 0.1 * np.random.standard_normal((1, 1, E))),
            "Wq_trop": bf(np.random.standard_normal((DK, DK))),
            "Wk_trop": bf(np.random.standard_normal((DK, DK))),
            "Wv_trop": bf(np.random.standard_normal((DK, DK)))}


def reference(x, Wq_words, Wq_scales, Wk_words, Wk_scales, Wv_words, Wv_scales, lam, Wq_trop, Wk_trop, Wv_trop):
    xq = mxq(f64(x), 2, "e4m3")
    lam = f64(lam)
    q = tropical_linear(split_heads(proj(xq, Wq_words, Wq_scales, lam)), f64(Wq_trop))
    k = tropical_linear(split_heads(proj(xq, Wk_words, Wk_scales, lam)), f64(Wk_trop))
    v = tropical_linear(split_heads(proj(xq, Wv_words, Wv_scales, lam)), f64(Wv_trop))
    return q, k, v

@@ -1,0 +1,206 @@
+import concourse.mybir as mybir
+from concourse.masks import make_identity
+
+F32 = mybir.dt.float32
+BF16 = mybir.dt.bfloat16
+I32 = mybir.dt.int32
+U32 = mybir.dt.uint32
+U8 = mybir.dt.uint8
+FP8X4 = mybir.dt.float8_e4m3fn_x4
+ACT = mybir.ActivationFunctionType
+ALU = mybir.AluOpType
+
+P = 128
+TOKENS = 16 * 256
+BATCH_LEN = 256
+D = 512
+HEADS = 4
+DK = 64
+E = HEADS * DK
+PROJ = 3
+CHUNK = 512
+BLOCKS = CHUNK // P
+N_CHUNKS = TOKENS // CHUNK
+PAIRS = E // P
+TILES = PROJ * PAIRS
+
+FLOPS = 2 * TOKENS * D * PROJ * E + 2 * TOKENS * PROJ * E * DK
+
+
+def tile_tropicalattention_pa_t_kernel(
+    tc,
+    x,
+    Wq_words,
+    Wq_scales,
+    Wk_words,
+    Wk_scales,
+    Wv_words,
+    Wv_scales,
+    lam,
+    Wq_trop,
+    Wk_trop,
+    Wv_trop,
+    out_0,
+    out_1,
+    out_2,
+):
+    nc = tc.nc
+    x_rows = x.flatten_outer_dims()
+    outs = [out_0, out_1, out_2]
+
+    with (
+        tc.tile_pool(name="const", bufs=1) as const,
+        tc.tile_pool(name="tokens", bufs=2) as tokens,
+        tc.tile_pool(name="logs", bufs=2 * TILES) as logs,
+        tc.tile_pool(name="sums", bufs=6) as sums,
+        tc.tile_pool(name="results", bufs=3) as results,
+        tc.psum_pool(name="psum_small", bufs=1) as psum_small,
+        tc.psum_pool(name="psum_sums", bufs=6) as psum_sums,
+    ):
+        ident = const.tile([P, P], F32)
+        make_identity(nc, ident[:])
+
+        w_codes = const.tile([P, PROJ * E], U32, align_bytes=64)
+        w_scales = const.tile([P, PROJ * E], U8, align_bytes=64)
+        nc.vector.memset(w_scales[:].bitcast(I32), 0)
+        weights = [(Wq_words, Wq_scales), (Wk_words, Wk_scales), (Wv_words, Wv_scales)]
+        for j, (words, scales) in enumerate(weights):
+            cols = slice(j * E, (j + 1) * E)
+            nc.sync.dma_start(
+                out=w_codes[:, cols].bitcast(I32),
+                in_=words[0].rearrange("p n t -> p (n t)").bitcast(I32),
+            )
+            for quadrant in range(4):
+                nc.sync.dma_start(
+                    out=w_scales[32 * quadrant : 32 * quadrant + 4, cols].bitcast(I32),
+                    in_=scales[0, 4 * quadrant : 4 * quadrant + 4, :].bitcast(I32),
+                )
+
+        rows_bf = const.tile([P, 2, P], BF16)
+        nc.vector.memset(rows_bf[:], 0.0)
+        for half in range(2):
+            cols = slice(half * DK, (half + 1) * DK)
+            nc.sync.dma_start(out=rows_bf[0:DK, 0, cols], in_=Wq_trop)
+            nc.sync.dma_start(out=rows_bf[DK:P, 0, cols], in_=Wk_trop)
+            nc.sync.dma_start(out=rows_bf[0:DK, 1, cols], in_=Wv_trop)
+        nc.sync.dma_start(
+            out=rows_bf[DK : DK + PAIRS, 1, :],
+            in_=lam.rearrange("a b (r n) -> (a b r) n", r=PAIRS),
+        )
+        rows_f32 = const.tile([P, 2, P], F32)
+        nc.vector.tensor_copy(out=rows_f32[:], in_=rows_bf[:])
+        turned_ps = psum_small.tile([P, 2, P], F32, tag="turn")
+        for square in range(2):
+            nc.tensor.transpose(turned_ps[:, square, :], rows_f32[:, square, :], ident[:])
+        turned = const.tile([P, 2 * P], F32)
+        nc.vector.tensor_copy(out=turned[:], in_=turned_ps[:].rearrange("p s c -> p (s c)"))
+        lam_col = PROJ * DK
+        offset = const.tile([P, TILES, DK], F32)
+        for j in range(PROJ):
+            for pair in range(PAIRS):
+                nc.vector.tensor_scalar(
+                    out=offset[:, j * PAIRS + pair, :],
+                    in0=turned[:, j * DK : (j + 1) * DK],
+                    scalar1=turned[:, lam_col + pair : lam_col + pair + 1],
+                    scalar2=None,
+                    op0=ALU.subtract,
+                )
+
+        def quantise_chunk(c):
+            x_sb = tokens.tile([P, BLOCKS, D], BF16)
+            nc.sync.dma_start(
+                out=x_sb[:],
+                in_=x_rows[c * CHUNK : (c + 1) * CHUNK, :].rearrange("(b p) k -> p b k", p=P),
+            )
+            grouped = tokens.tile([P, CHUNK, 4], BF16, align_bytes=64)
+            grouped_words = grouped[:].bitcast(F32)
+            for half in range(2):
+                turn = psum_small.tile([P, 2, 2, P], F32, tag="turn")
+                for b in range(2):
+                    x_words = x_sb[:, 2 * half + b, :].bitcast(F32)
+                    for u in range(2):
+                        nc.tensor.transpose(turn[:, b, u, :], x_words[:, u : D // 2 : 2], ident[:])
+                nc.scalar.copy(
+                    out=grouped_words[:, half * 2 * P : (half + 1) * 2 * P, :].rearrange(
+                        "p (b r) u -> p b r u", b=2
+                    ),
+                    in_=turn[:].rearrange("p b u r -> p b r u"),
+                )
+            x_codes = tokens.tile([P, CHUNK], U32, align_bytes=64)
+            x_scales = tokens.tile([P, CHUNK], U8, align_bytes=64)
+            nc.vector.quantize_mx(
+                out=x_codes[:].bitcast(FP8X4),
+                scales=x_scales[:],
+                in_=grouped[:].rearrange("p r t -> p (r t)"),
+            )
+            return x_codes, x_scales
+
+        def log_features(x_codes, x_scales, t):
+            cols = slice(t * P, (t + 1) * P)
+            z = psum_small.tile([P, CHUNK], F32, tag="z")
+            nc.tensor.matmul_mx(
+                out=z[:],
+                lhsT=w_codes[:, cols].bitcast(FP8X4),
+                lhsT_scale=w_scales[:, cols],
+                rhs=x_codes[:].bitcast(FP8X4),
+                rhs_scale=x_scales[:],
+                start=True,
+                stop=True,
+            )
+            positive = tokens.tile([P, CHUNK], F32)
+            nc.scalar.activation(out=positive[:], in_=z[:], func=ACT.Relu)
+            log_tile = logs.tile([P, CHUNK], F32)
+            nc.scalar.activation(out=log_tile[:], in_=positive[:], func=ACT.Ln, bias=1.0, scale=1.0)
+            return log_tile
+
+        def tropical(log_tile, t, y):
+            pair = t % PAIRS
+            for o in range(DK):
+                shift = offset[:, t, o : o + 1]
+                shifted = sums.tile([P, CHUNK], F32)
+                if o % 3 == 2:
+                    nc.gpsimd.tensor_scalar(
+                        out=shifted[:], in0=log_tile[:], scalar1=shift, scalar2=1.0,
+                        op0=ALU.add, op1=ALU.mult,
+                    )
+                else:
+                    nc.scalar.activation(
+                        out=shifted[:], in_=log_tile[:], func=ACT.Identity, bias=shift, scale=1.0
+                    )
+                by_token = psum_sums.tile([P, BLOCKS, P], F32)
+                for b in range(BLOCKS):
+                    nc.tensor.transpose(by_token[:, b, :], shifted[:, b * P : (b + 1) * P], ident[:])
+                nc.vector.tensor_reduce(
+                    out=y[:, :, 2 * pair : 2 * pair + 2, o],
+                    in_=by_token[:].rearrange("p b (h i) -> p b h i", h=2),
+                    axis=mybir.AxisListType.X,
+                    op=ALU.max,
+                )
+
+        def store(c, j, y):
+            for b in range(BLOCKS):
+                first = c * CHUNK + b * P
+                batch, l0 = first // BATCH_LEN, first % BATCH_LEN
+                nc.sync.dma_start(
+                    out=outs[j][batch * HEADS : (batch + 1) * HEADS, l0 : l0 + P, :].rearrange(
+                        "h l o -> l h o"
+                    ),
+                    in_=y[:, b, :, :],
+                )
+
+        codes = quantise_chunk(0)
+        log_tiles = [log_features(codes[0], codes[1], t) for t in range(TILES)]
+        for c in range(N_CHUNKS):
+            more = c + 1 < N_CHUNKS
+            if more:
+                codes = quantise_chunk(c + 1)
+            next_tiles = []
+            for j in range(PROJ):
+                y = results.tile([P, BLOCKS, HEADS, DK], F32)
+                for pair in range(PAIRS):
+                    t = j * PAIRS + pair
+                    tropical(log_tiles[t], t, y)
+                    if more:
+                        next_tiles.append(log_features(codes[0], codes[1], t))
+                store(c, j, y)
+            log_tiles = next_tiles

@@ -9,6 +9,7 @@ U8 = mybir.dt.uint8
 FP8X4 = mybir.dt.float8_e4m3fn_x4
 ACT = mybir.ActivationFunctionType
 ALU = mybir.AluOpType
+X_AXIS = mybir.AxisListType.X
 
 P = 128
 TOKENS = 16 * 256
@@ -16,13 +17,15 @@ BATCH_LEN = 256
 D = 512
 HEADS = 4
 DK = 64
+HALF = DK // 2
 E = HEADS * DK
 PROJ = 3
-CHUNK = 512
+BANK = 512
+CHUNK = 1024
 BLOCKS = CHUNK // P
+BANK_BLOCKS = BANK // P
 N_CHUNKS = TOKENS // CHUNK
-PAIRS = E // P
-TILES = PROJ * PAIRS
+LOG_LIMIT = 89.0
 
 FLOPS = 2 * TOKENS * D * PROJ * E + 2 * TOKENS * PROJ * E * DK
 
@@ -51,77 +54,33 @@ def tile_tropicalattention_pa_t_kernel(
     with (
         tc.tile_pool(name="const", bufs=1) as const,
         tc.tile_pool(name="tokens", bufs=2) as tokens,
-        tc.tile_pool(name="logs", bufs=2 * TILES) as logs,
-        tc.tile_pool(name="sums", bufs=6) as sums,
-        tc.tile_pool(name="results", bufs=3) as results,
+        tc.tile_pool(name="logs", bufs=4) as logs,
+        tc.tile_pool(name="sums", bufs=4) as sums,
+        tc.tile_pool(name="results", bufs=2) as results,
         tc.psum_pool(name="psum_small", bufs=1) as psum_small,
-        tc.psum_pool(name="psum_sums", bufs=6) as psum_sums,
+        tc.psum_pool(name="psum_sums", bufs=5) as psum_sums,
     ):
         ident = const.tile([P, P], F32)
         make_identity(nc, ident[:])
 
-        w_codes = const.tile([P, PROJ * E], U32, align_bytes=64)
-        w_scales = const.tile([P, PROJ * E], U8, align_bytes=64)
-        nc.vector.memset(w_scales[:].bitcast(I32), 0)
-        weights = [(Wq_words, Wq_scales), (Wk_words, Wk_scales), (Wv_words, Wv_scales)]
-        for j, (words, scales) in enumerate(weights):
-            cols = slice(j * E, (j + 1) * E)
-            nc.sync.dma_start(
-                out=w_codes[:, cols].bitcast(I32),
-                in_=words[0].rearrange("p n t -> p (n t)").bitcast(I32),
-            )
-            for quadrant in range(4):
-                nc.sync.dma_start(
-                    out=w_scales[32 * quadrant : 32 * quadrant + 4, cols].bitcast(I32),
-                    in_=scales[0, 4 * quadrant : 4 * quadrant + 4, :].bitcast(I32),
-                )
-
-        rows_bf = const.tile([P, 2, P], BF16)
-        nc.vector.memset(rows_bf[:], 0.0)
-        for half in range(2):
-            cols = slice(half * DK, (half + 1) * DK)
-            nc.sync.dma_start(out=rows_bf[0:DK, 0, cols], in_=Wq_trop)
-            nc.sync.dma_start(out=rows_bf[DK:P, 0, cols], in_=Wk_trop)
-            nc.sync.dma_start(out=rows_bf[0:DK, 1, cols], in_=Wv_trop)
-        nc.sync.dma_start(
-            out=rows_bf[DK : DK + PAIRS, 1, :],
-            in_=lam.rearrange("a b (r n) -> (a b r) n", r=PAIRS),
-        )
-        rows_f32 = const.tile([P, 2, P], F32)
-        nc.vector.tensor_copy(out=rows_f32[:], in_=rows_bf[:])
-        turned_ps = psum_small.tile([P, 2, P], F32, tag="turn")
-        for square in range(2):
-            nc.tensor.transpose(turned_ps[:, square, :], rows_f32[:, square, :], ident[:])
-        turned = const.tile([P, 2 * P], F32)
-        nc.vector.tensor_copy(out=turned[:], in_=turned_ps[:].rearrange("p s c -> p (s c)"))
-        lam_col = PROJ * DK
-        offset = const.tile([P, TILES, DK], F32)
-        for j in range(PROJ):
-            for pair in range(PAIRS):
-                nc.vector.tensor_scalar(
-                    out=offset[:, j * PAIRS + pair, :],
-                    in0=turned[:, j * DK : (j + 1) * DK],
-                    scalar1=turned[:, lam_col + pair : lam_col + pair + 1],
-                    scalar2=None,
-                    op0=ALU.subtract,
-                )
-
-        def quantise_chunk(c):
+        def quantise_chunk(chunk):
             x_sb = tokens.tile([P, BLOCKS, D], BF16)
             nc.sync.dma_start(
                 out=x_sb[:],
-                in_=x_rows[c * CHUNK : (c + 1) * CHUNK, :].rearrange("(b p) k -> p b k", p=P),
+                in_=x_rows[chunk * CHUNK : (chunk + 1) * CHUNK, :].rearrange(
+                    "(b p) k -> p b k", p=P
+                ),
             )
             grouped = tokens.tile([P, CHUNK, 4], BF16, align_bytes=64)
             grouped_words = grouped[:].bitcast(F32)
-            for half in range(2):
+            for two in range(BLOCKS // 2):
                 turn = psum_small.tile([P, 2, 2, P], F32, tag="turn")
                 for b in range(2):
-                    x_words = x_sb[:, 2 * half + b, :].bitcast(F32)
+                    x_words = x_sb[:, 2 * two + b, :].bitcast(F32)
                     for u in range(2):
                         nc.tensor.transpose(turn[:, b, u, :], x_words[:, u : D // 2 : 2], ident[:])
-                nc.scalar.copy(
-                    out=grouped_words[:, half * 2 * P : (half + 1) * 2 * P, :].rearrange(
+                nc.vector.tensor_copy(
+                    out=grouped_words[:, two * 2 * P : (two + 1) * 2 * P, :].rearrange(
                         "p (b r) u -> p b r u", b=2
                     ),
                     in_=turn[:].rearrange("p b u r -> p b r u"),
@@ -135,51 +94,145 @@ def tile_tropicalattention_pa_t_kernel(
             )
             return x_codes, x_scales
 
-        def log_features(x_codes, x_scales, t):
-            cols = slice(t * P, (t + 1) * P)
-            z = psum_small.tile([P, CHUNK], F32, tag="z")
-            nc.tensor.matmul_mx(
-                out=z[:],
-                lhsT=w_codes[:, cols].bitcast(FP8X4),
-                lhsT_scale=w_scales[:, cols],
-                rhs=x_codes[:].bitcast(FP8X4),
-                rhs_scale=x_scales[:],
-                start=True,
-                stop=True,
+        codes = quantise_chunk(0)
+
+        w_codes = const.tile([P, PROJ, 2, P], U32, align_bytes=64)
+        w_scales = const.tile([P, PROJ, 2, P], U8, align_bytes=64)
+        nc.vector.memset(w_scales[:].bitcast(I32), 0)
+        weights = [(Wq_words, Wq_scales), (Wk_words, Wk_scales), (Wv_words, Wv_scales)]
+        for j, (words, scales) in enumerate(weights):
+            words_by_half = (
+                words[0]
+                .rearrange("p n t -> p (n t)")
+                .bitcast(I32)
+                .rearrange("p (h a i) -> p a h i", a=2, i=HALF)
             )
-            positive = tokens.tile([P, CHUNK], F32)
-            nc.scalar.activation(out=positive[:], in_=z[:], func=ACT.Relu)
-            log_tile = logs.tile([P, CHUNK], F32)
-            nc.scalar.activation(out=log_tile[:], in_=positive[:], func=ACT.Ln, bias=1.0, scale=1.0)
-            return log_tile
-
-        def tropical(log_tile, t, y):
-            pair = t % PAIRS
-            for o in range(DK):
-                shift = offset[:, t, o : o + 1]
-                shifted = sums.tile([P, CHUNK], F32)
-                if o % 3 == 2:
-                    nc.gpsimd.tensor_scalar(
-                        out=shifted[:], in0=log_tile[:], scalar1=shift, scalar2=1.0,
-                        op0=ALU.add, op1=ALU.mult,
-                    )
-                else:
-                    nc.scalar.activation(
-                        out=shifted[:], in_=log_tile[:], func=ACT.Identity, bias=shift, scale=1.0
-                    )
-                by_token = psum_sums.tile([P, BLOCKS, P], F32)
-                for b in range(BLOCKS):
-                    nc.tensor.transpose(by_token[:, b, :], shifted[:, b * P : (b + 1) * P], ident[:])
-                nc.vector.tensor_reduce(
-                    out=y[:, :, 2 * pair : 2 * pair + 2, o],
-                    in_=by_token[:].rearrange("p b (h i) -> p b h i", h=2),
-                    axis=mybir.AxisListType.X,
-                    op=ALU.max,
+            for a in range(2):
+                nc.sync.dma_start(
+                    out=w_codes[:, j, a, :].bitcast(I32).rearrange("p (h i) -> p h i", h=HEADS),
+                    in_=words_by_half[:, a, :, :],
                 )
+            for quadrant in range(4):
+                rows_by_half = (
+                    scales[0, 4 * quadrant : 4 * quadrant + 4, :]
+                    .bitcast(I32)
+                    .rearrange("r (h a w) -> r a h w", a=2, w=HALF // 4)
+                )
+                for a in range(2):
+                    nc.sync.dma_start(
+                        out=w_scales[32 * quadrant : 32 * quadrant + 4, j, a, :]
+                        .bitcast(I32)
+                        .rearrange("r (h w) -> r h w", h=HEADS),
+                        in_=rows_by_half[:, a, :, :],
+                    )
 
-        def store(c, j, y):
+        t_rows = const.tile([P, 2, DK], BF16)
+        nc.sync.dma_start(out=t_rows[0:DK, 0, :], in_=Wq_trop)
+        nc.sync.dma_start(out=t_rows[DK:P, 0, :], in_=Wk_trop)
+        nc.sync.dma_start(out=t_rows[0:DK, 1, :], in_=Wv_trop)
+        nc.sync.dma_start(out=t_rows[DK:P, 1, :], in_=Wv_trop)
+        lam_rows = const.tile([P, E], BF16)
+        nc.sync.dma_start(
+            out=lam_rows[:], in_=lam.rearrange("a b n -> (a b n)").partition_broadcast(P)
+        )
+        c = const.tile([P, 2, HEADS, DK], F32)
+        for square in range(2):
+            nc.vector.tensor_tensor(
+                out=c[:, square, :, :],
+                in0=t_rows[:, square, :].unsqueeze(1).to_broadcast([P, HEADS, DK]),
+                in1=lam_rows[:].rearrange("p (h i) -> p h i", h=HEADS),
+                op=ALU.subtract,
+            )
+        c_floor = const.tile([P, 2, HEADS], F32)
+        nc.vector.tensor_reduce(out=c_floor[:], in_=c[:], axis=X_AXIS, op=ALU.max)
+        nc.vector.tensor_scalar(
+            out=c_floor[:], in0=c_floor[:], scalar1=-LOG_LIMIT, scalar2=None, op0=ALU.add
+        )
+        nc.vector.tensor_tensor(
+            out=c[:],
+            in0=c[:],
+            in1=c_floor[:].unsqueeze(3).to_broadcast([P, 2, HEADS, DK]),
+            op=ALU.max,
+        )
+        c_rows = const.tile([P, 2, 2, HEADS, HALF], F32)
+        nc.vector.tensor_copy(out=c_rows[:, 0, :, :, :], in_=c[:, :, :, 0:HALF])
+        nc.vector.tensor_sub(
+            out=c_rows[:, 1, :, :, :], in0=c[:, :, :, HALF:DK], in1=c[:, :, :, 0:HALF]
+        )
+        c_turned = psum_small.tile([P, 2, 2, P], F32, tag="turn")
+        for kind in range(2):
+            for square in range(2):
+                nc.tensor.transpose(
+                    c_turned[:, kind, square, :],
+                    c_rows[:, kind, square, :, :].rearrange("p h i -> p (h i)"),
+                    ident[:],
+                )
+        c_cols = const.tile([P, 2, 2 * P], F32)
+        nc.vector.tensor_copy(out=c_cols[:], in_=c_turned[:].rearrange("p k s o -> p k (s o)"))
+
+        def log_half(x_codes, x_scales, j, a, g):
+            grown = tokens.tile([P, CHUNK], F32)
+            for first in range(0, CHUNK, BANK):
+                z = psum_small.tile([P, BANK], F32, tag="z", bufs=2)
+                nc.tensor.matmul_mx(
+                    out=z[:],
+                    lhsT=w_codes[:, j, a, :].bitcast(FP8X4),
+                    lhsT_scale=w_scales[:, j, a, :],
+                    rhs=x_codes[:, first : first + BANK].bitcast(FP8X4),
+                    rhs_scale=x_scales[:, first : first + BANK],
+                    start=True,
+                    stop=True,
+                )
+                nc.vector.tensor_scalar(
+                    out=grown[:, first : first + BANK], in0=z[:], scalar1=0.0, scalar2=1.0,
+                    op0=ALU.max, op1=ALU.add,
+                )
+            nc.scalar.activation(out=g[:], in_=grown[:], func=ACT.Ln)
+
+        def log_features(x_codes, x_scales, j):
+            g_lo = logs.tile([P, CHUNK], F32)
+            log_half(x_codes, x_scales, j, 0, g_lo)
+            g_hi = tokens.tile([P, CHUNK], F32)
+            log_half(x_codes, x_scales, j, 1, g_hi)
+            g_step = logs.tile([P, CHUNK], F32)
+            nc.vector.tensor_sub(out=g_step[:], in0=g_hi[:], in1=g_lo[:])
+            return g_lo, g_step
+
+        def tropical(g_lo, g_step, j, y):
+            for o in range(DK):
+                col = j * DK + o
+                sum_lo = sums.tile([P, CHUNK], F32)
+                nc.gpsimd.tensor_scalar(
+                    out=sum_lo[:], in0=g_lo[:], scalar1=c_cols[:, 0, col : col + 1], scalar2=1.0,
+                    op0=ALU.add, op1=ALU.mult,
+                )
+                excess = sums.tile([P, CHUNK], F32)
+                nc.scalar.activation(
+                    out=excess[:], in_=g_step[:], func=ACT.Relu,
+                    bias=c_cols[:, 1, col : col + 1], scale=1.0,
+                )
+                for b0 in range(0, BLOCKS, BANK_BLOCKS):
+                    pair_max = psum_sums.tile([P, BANK_BLOCKS, P], F32)
+                    for b in range(BANK_BLOCKS):
+                        cols = slice((b0 + b) * P, (b0 + b + 1) * P)
+                        nc.tensor.matmul(
+                            out=pair_max[:, b, :], lhsT=sum_lo[:, cols], rhs=ident[:],
+                            start=True, stop=False, is_transpose=True,
+                        )
+                        nc.tensor.matmul(
+                            out=pair_max[:, b, :], lhsT=excess[:, cols], rhs=ident[:],
+                            start=False, stop=True, is_transpose=True,
+                        )
+                    nc.vector.tensor_reduce(
+                        out=y[:, b0 : b0 + BANK_BLOCKS, :, o],
+                        in_=pair_max[:].rearrange("p b (h i) -> p b h i", h=HEADS),
+                        axis=X_AXIS,
+                        op=ALU.max,
+                    )
+
+        def store(chunk, j, y):
             for b in range(BLOCKS):
-                first = c * CHUNK + b * P
+                first = chunk * CHUNK + b * P
                 batch, l0 = first // BATCH_LEN, first % BATCH_LEN
                 nc.sync.dma_start(
                     out=outs[j][batch * HEADS : (batch + 1) * HEADS, l0 : l0 + P, :].rearrange(
@@ -188,19 +241,16 @@ def tile_tropicalattention_pa_t_kernel(
                     in_=y[:, b, :, :],
                 )
 
-        codes = quantise_chunk(0)
-        log_tiles = [log_features(codes[0], codes[1], t) for t in range(TILES)]
-        for c in range(N_CHUNKS):
-            more = c + 1 < N_CHUNKS
+        features = [log_features(codes[0], codes[1], j) for j in range(PROJ)]
+        for chunk in range(N_CHUNKS):
+            more = chunk + 1 < N_CHUNKS
             if more:
-                codes = quantise_chunk(c + 1)
-            next_tiles = []
+                codes = quantise_chunk(chunk + 1)
+            next_features = []
             for j in range(PROJ):
                 y = results.tile([P, BLOCKS, HEADS, DK], F32)
-                for pair in range(PAIRS):
-                    t = j * PAIRS + pair
-                    tropical(log_tiles[t], t, y)
-                    if more:
-                        next_tiles.append(log_features(codes[0], codes[1], t))
-                store(c, j, y)
-            log_tiles = next_tiles
+                tropical(features[j][0], features[j][1], j, y)
+                if more:
+                    next_features.append(log_features(codes[0], codes[1], j))
+                store(chunk, j, y)
+            features = next_features

@@ -57,8 +57,8 @@ def tile_tropicalattention_pa_t_kernel(
         tc.tile_pool(name="logs", bufs=4) as logs,
         tc.tile_pool(name="sums", bufs=4) as sums,
         tc.tile_pool(name="results", bufs=2) as results,
-        tc.psum_pool(name="psum_small", bufs=1) as psum_small,
-        tc.psum_pool(name="psum_sums", bufs=5) as psum_sums,
+        tc.psum_pool(name="psum_small", bufs=2) as psum_small,
+        tc.psum_pool(name="psum_sums", bufs=4) as psum_sums,
     ):
         ident = const.tile([P, P], F32)
         make_identity(nc, ident[:])
@@ -127,12 +127,12 @@ def tile_tropicalattention_pa_t_kernel(
                     )
 
         t_rows = const.tile([P, 2, DK], BF16)
-        nc.sync.dma_start(out=t_rows[0:DK, 0, :], in_=Wq_trop)
-        nc.sync.dma_start(out=t_rows[DK:P, 0, :], in_=Wk_trop)
-        nc.sync.dma_start(out=t_rows[0:DK, 1, :], in_=Wv_trop)
-        nc.sync.dma_start(out=t_rows[DK:P, 1, :], in_=Wv_trop)
+        nc.scalar.dma_start(out=t_rows[0:DK, 0, :], in_=Wq_trop)
+        nc.scalar.dma_start(out=t_rows[DK:P, 0, :], in_=Wk_trop)
+        nc.scalar.dma_start(out=t_rows[0:DK, 1, :], in_=Wv_trop)
+        nc.scalar.dma_start(out=t_rows[DK:P, 1, :], in_=Wv_trop)
         lam_rows = const.tile([P, E], BF16)
-        nc.sync.dma_start(
+        nc.scalar.dma_start(
             out=lam_rows[:], in_=lam.rearrange("a b n -> (a b n)").partition_broadcast(P)
         )
         c = const.tile([P, 2, HEADS, DK], F32)
@@ -173,7 +173,7 @@ def tile_tropicalattention_pa_t_kernel(
         def log_half(x_codes, x_scales, j, a, g):
             grown = tokens.tile([P, CHUNK], F32)
             for first in range(0, CHUNK, BANK):
-                z = psum_small.tile([P, BANK], F32, tag="z", bufs=2)
+                z = psum_small.tile([P, BANK], F32, tag="z")
                 nc.tensor.matmul_mx(
                     out=z[:],
                     lhsT=w_codes[:, j, a, :].bitcast(FP8X4),
@@ -189,23 +189,20 @@ def tile_tropicalattention_pa_t_kernel(
                 )
             nc.scalar.activation(out=g[:], in_=grown[:], func=ACT.Ln)
 
-        def log_features(x_codes, x_scales, j):
-            g_lo = logs.tile([P, CHUNK], F32)
-            log_half(x_codes, x_scales, j, 0, g_lo)
-            g_hi = tokens.tile([P, CHUNK], F32)
-            log_half(x_codes, x_scales, j, 1, g_hi)
-            g_step = logs.tile([P, CHUNK], F32)
-            nc.vector.tensor_sub(out=g_step[:], in0=g_hi[:], in1=g_lo[:])
-            return g_lo, g_step
-
-        def tropical(g_lo, g_step, j, y):
-            for o in range(DK):
+        def tropical(g_lo, g_step, j, o_range, y):
+            for o in o_range:
                 col = j * DK + o
                 sum_lo = sums.tile([P, CHUNK], F32)
-                nc.gpsimd.tensor_scalar(
-                    out=sum_lo[:], in0=g_lo[:], scalar1=c_cols[:, 0, col : col + 1], scalar2=1.0,
-                    op0=ALU.add, op1=ALU.mult,
-                )
+                if o % 8 == 7:
+                    nc.scalar.activation(
+                        out=sum_lo[:], in_=g_lo[:], func=ACT.Identity,
+                        bias=c_cols[:, 0, col : col + 1], scale=1.0,
+                    )
+                else:
+                    nc.gpsimd.tensor_scalar(
+                        out=sum_lo[:], in0=g_lo[:], scalar1=c_cols[:, 0, col : col + 1],
+                        scalar2=1.0, op0=ALU.add, op1=ALU.mult,
+                    )
                 excess = sums.tile([P, CHUNK], F32)
                 nc.scalar.activation(
                     out=excess[:], in_=g_step[:], func=ACT.Relu,
@@ -241,16 +238,36 @@ def tile_tropicalattention_pa_t_kernel(
                     in_=y[:, b, :, :],
                 )
 
-        features = [log_features(codes[0], codes[1], j) for j in range(PROJ)]
-        for chunk in range(N_CHUNKS):
-            more = chunk + 1 < N_CHUNKS
+        quarters = [range(q * DK // 4, (q + 1) * DK // 4) for q in range(4)]
+        next_codes = codes
+        g_lo = logs.tile([P, CHUNK], F32)
+        log_half(codes[0], codes[1], 0, 0, g_lo)
+        g_hi = tokens.tile([P, CHUNK], F32)
+        log_half(codes[0], codes[1], 0, 1, g_hi)
+        g_step = logs.tile([P, CHUNK], F32)
+        nc.vector.tensor_sub(out=g_step[:], in0=g_hi[:], in1=g_lo[:])
+        for stage in range(N_CHUNKS * PROJ):
+            chunk, j = divmod(stage, PROJ)
+            next_j = (j + 1) % PROJ
+            more = stage + 1 < N_CHUNKS * PROJ
+            if next_j == 0:
+                codes = next_codes
+            y = results.tile([P, BLOCKS, HEADS, DK], F32)
+
+            tropical(g_lo, g_step, j, quarters[0], y)
             if more:
-                codes = quantise_chunk(chunk + 1)
-            next_features = []
-            for j in range(PROJ):
-                y = results.tile([P, BLOCKS, HEADS, DK], F32)
-                tropical(features[j][0], features[j][1], j, y)
-                if more:
-                    next_features.append(log_features(codes[0], codes[1], j))
-                store(chunk, j, y)
-            features = next_features
+                next_lo = logs.tile([P, CHUNK], F32, tag="g_lo")
+                log_half(codes[0], codes[1], next_j, 0, next_lo)
+            tropical(g_lo, g_step, j, quarters[1], y)
+            if more:
+                g_hi = tokens.tile([P, CHUNK], F32)
+                log_half(codes[0], codes[1], next_j, 1, g_hi)
+                next_step = logs.tile([P, CHUNK], F32, tag="g_step")
+                nc.vector.tensor_sub(out=next_step[:], in0=g_hi[:], in1=next_lo[:])
+            tropical(g_lo, g_step, j, quarters[2], y)
+            if j == 0 and chunk + 1 < N_CHUNKS:
+                next_codes = quantise_chunk(chunk + 1)
+            tropical(g_lo, g_step, j, quarters[3], y)
+            store(chunk, j, y)
+            if more:
+                g_lo, g_step = next_lo, next_step

@@ -55,7 +55,7 @@ def tile_tropicalattention_pa_t_kernel(
         tc.tile_pool(name="const", bufs=1) as const,
         tc.tile_pool(name="tokens", bufs=2) as tokens,
         tc.tile_pool(name="logs", bufs=4) as logs,
-        tc.tile_pool(name="sums", bufs=4) as sums,
+        tc.tile_pool(name="sums", bufs=6) as sums,
         tc.tile_pool(name="results", bufs=2) as results,
         tc.psum_pool(name="psum_small", bufs=2) as psum_small,
         tc.psum_pool(name="psum_sums", bufs=4) as psum_sums,
@@ -192,8 +192,13 @@ def tile_tropicalattention_pa_t_kernel(
         def tropical(g_lo, g_step, j, o_range, y):
             for o in o_range:
                 col = j * DK + o
+                excess = sums.tile([P, CHUNK], F32)
+                nc.scalar.activation(
+                    out=excess[:], in_=g_step[:], func=ACT.Relu,
+                    bias=c_cols[:, 1, col : col + 1], scale=1.0,
+                )
                 sum_lo = sums.tile([P, CHUNK], F32)
-                if o % 8 == 7:
+                if o % 8 == 3:
                     nc.scalar.activation(
                         out=sum_lo[:], in_=g_lo[:], func=ACT.Identity,
                         bias=c_cols[:, 0, col : col + 1], scale=1.0,
@@ -203,22 +208,23 @@ def tile_tropicalattention_pa_t_kernel(
                         out=sum_lo[:], in0=g_lo[:], scalar1=c_cols[:, 0, col : col + 1],
                         scalar2=1.0, op0=ALU.add, op1=ALU.mult,
                     )
-                excess = sums.tile([P, CHUNK], F32)
-                nc.scalar.activation(
-                    out=excess[:], in_=g_step[:], func=ACT.Relu,
-                    bias=c_cols[:, 1, col : col + 1], scale=1.0,
-                )
+                whole = o % 16 == 15
+                if whole:
+                    nc.gpsimd.tensor_tensor(
+                        out=excess[:], in0=excess[:], in1=sum_lo[:], op=ALU.add
+                    )
                 for b0 in range(0, BLOCKS, BANK_BLOCKS):
                     pair_max = psum_sums.tile([P, BANK_BLOCKS, P], F32)
                     for b in range(BANK_BLOCKS):
                         cols = slice((b0 + b) * P, (b0 + b + 1) * P)
-                        nc.tensor.matmul(
-                            out=pair_max[:, b, :], lhsT=sum_lo[:, cols], rhs=ident[:],
-                            start=True, stop=False, is_transpose=True,
-                        )
+                        if not whole:
+                            nc.tensor.matmul(
+                                out=pair_max[:, b, :], lhsT=sum_lo[:, cols], rhs=ident[:],
+                                start=True, stop=False, is_transpose=True,
+                            )
                         nc.tensor.matmul(
                             out=pair_max[:, b, :], lhsT=excess[:, cols], rhs=ident[:],
-                            start=False, stop=True, is_transpose=True,
+                            start=whole, stop=True, is_transpose=True,
                         )
                     nc.vector.tensor_reduce(
                         out=y[:, b0 : b0 + BANK_BLOCKS, :, o],

@@ -21,10 +21,15 @@ HALF = DK // 2
 E = HEADS * DK
 PROJ = 3
 BANK = 512
-CHUNK = 1024
+CHUNK = 2048
 BLOCKS = CHUNK // P
 BANK_BLOCKS = BANK // P
 N_CHUNKS = TOKENS // CHUNK
+X_PART = 1024
+X_BLOCKS = X_PART // P
+PARTS = CHUNK // X_PART
+SCALAR_ADDS_EVERY = 6
+WHOLE_SUM_EVERY = 11
 LOG_LIMIT = 89.0
 
 FLOPS = 2 * TOKENS * D * PROJ * E + 2 * TOKENS * PROJ * E * DK
@@ -54,8 +59,9 @@ def tile_tropicalattention_pa_t_kernel(
     with (
         tc.tile_pool(name="const", bufs=1) as const,
         tc.tile_pool(name="tokens", bufs=2) as tokens,
-        tc.tile_pool(name="logs", bufs=4) as logs,
-        tc.tile_pool(name="sums", bufs=6) as sums,
+        tc.tile_pool(name="coded", bufs=TOKENS // X_PART) as coded,
+        tc.tile_pool(name="logs", bufs=2) as logs,
+        tc.tile_pool(name="sums", bufs=4) as sums,
         tc.tile_pool(name="results", bufs=2) as results,
         tc.psum_pool(name="psum_small", bufs=2) as psum_small,
         tc.psum_pool(name="psum_sums", bufs=4) as psum_sums,
@@ -63,38 +69,50 @@ def tile_tropicalattention_pa_t_kernel(
         ident = const.tile([P, P], F32)
         make_identity(nc, ident[:])
 
-        def quantise_chunk(chunk):
-            x_sb = tokens.tile([P, BLOCKS, D], BF16)
+        codes = []
+
+        def x_steps(part):
+            x_sb = tokens.tile([P, X_BLOCKS, D], BF16)
             nc.sync.dma_start(
                 out=x_sb[:],
-                in_=x_rows[chunk * CHUNK : (chunk + 1) * CHUNK, :].rearrange(
+                in_=x_rows[part * X_PART : (part + 1) * X_PART, :].rearrange(
                     "(b p) k -> p b k", p=P
                 ),
             )
-            grouped = tokens.tile([P, CHUNK, 4], BF16, align_bytes=64)
+            grouped = tokens.tile([P, X_PART, 4], BF16, align_bytes=64)
             grouped_words = grouped[:].bitcast(F32)
-            for two in range(BLOCKS // 2):
-                turn = psum_small.tile([P, 2, 2, P], F32, tag="turn")
+            x_codes = coded.tile([P, X_PART], U32, align_bytes=64)
+            x_scales = coded.tile([P, X_PART], U8, align_bytes=64)
+            codes.append((x_codes, x_scales))
+
+            def turn_two_blocks(two):
+                turned = psum_small.tile([P, 2, 2, P], F32, tag="turned")
                 for b in range(2):
                     x_words = x_sb[:, 2 * two + b, :].bitcast(F32)
                     for u in range(2):
-                        nc.tensor.transpose(turn[:, b, u, :], x_words[:, u : D // 2 : 2], ident[:])
+                        nc.tensor.transpose(
+                            turned[:, b, u, :], x_words[:, u : D // 2 : 2], ident[:]
+                        )
                 nc.vector.tensor_copy(
                     out=grouped_words[:, two * 2 * P : (two + 1) * 2 * P, :].rearrange(
                         "p (b r) u -> p b r u", b=2
                     ),
-                    in_=turn[:].rearrange("p b u r -> p b r u"),
+                    in_=turned[:].rearrange("p b u r -> p b r u"),
                 )
-            x_codes = tokens.tile([P, CHUNK], U32, align_bytes=64)
-            x_scales = tokens.tile([P, CHUNK], U8, align_bytes=64)
-            nc.vector.quantize_mx(
-                out=x_codes[:].bitcast(FP8X4),
-                scales=x_scales[:],
-                in_=grouped[:].rearrange("p r t -> p (r t)"),
-            )
-            return x_codes, x_scales
 
-        codes = quantise_chunk(0)
+            def quantise():
+                nc.vector.quantize_mx(
+                    out=x_codes[:].bitcast(FP8X4),
+                    scales=x_scales[:],
+                    in_=grouped[:].rearrange("p r t -> p (r t)"),
+                )
+
+            return [lambda two=two: turn_two_blocks(two) for two in range(X_BLOCKS // 2)] + [
+                quantise
+            ]
+
+        for step in x_steps(0):
+            step()
 
         w_codes = const.tile([P, PROJ, 2, P], U32, align_bytes=64)
         w_scales = const.tile([P, PROJ, 2, P], U8, align_bytes=64)
@@ -159,7 +177,7 @@ def tile_tropicalattention_pa_t_kernel(
         nc.vector.tensor_sub(
             out=c_rows[:, 1, :, :, :], in0=c[:, :, :, HALF:DK], in1=c[:, :, :, 0:HALF]
         )
-        c_turned = psum_small.tile([P, 2, 2, P], F32, tag="turn")
+        c_turned = psum_small.tile([P, 2, 2, P], F32, tag="turned")
         for kind in range(2):
             for square in range(2):
                 nc.tensor.transpose(
@@ -170,71 +188,90 @@ def tile_tropicalattention_pa_t_kernel(
         c_cols = const.tile([P, 2, 2 * P], F32)
         nc.vector.tensor_copy(out=c_cols[:], in_=c_turned[:].rearrange("p k s o -> p k (s o)"))
 
-        def log_half(x_codes, x_scales, j, a, g):
-            grown = tokens.tile([P, CHUNK], F32)
-            for first in range(0, CHUNK, BANK):
-                z = psum_small.tile([P, BANK], F32, tag="z")
-                nc.tensor.matmul_mx(
-                    out=z[:],
-                    lhsT=w_codes[:, j, a, :].bitcast(FP8X4),
-                    lhsT_scale=w_scales[:, j, a, :],
-                    rhs=x_codes[:, first : first + BANK].bitcast(FP8X4),
-                    rhs_scale=x_scales[:, first : first + BANK],
-                    start=True,
-                    stop=True,
-                )
-                nc.vector.tensor_scalar(
-                    out=grown[:, first : first + BANK], in0=z[:], scalar1=0.0, scalar2=1.0,
-                    op0=ALU.max, op1=ALU.add,
-                )
-            nc.scalar.activation(out=g[:], in_=grown[:], func=ACT.Ln)
+        def log_steps(chunk, j):
+            g_lo = logs.tile([P, CHUNK], F32)
+            g_step = logs.tile([P, CHUNK], F32)
+            g_hi = tokens.tile([P, CHUNK], F32)
 
-        def tropical(g_lo, g_step, j, o_range, y):
-            for o in o_range:
-                col = j * DK + o
-                excess = sums.tile([P, CHUNK], F32)
-                nc.scalar.activation(
-                    out=excess[:], in_=g_step[:], func=ACT.Relu,
-                    bias=c_cols[:, 1, col : col + 1], scale=1.0,
-                )
-                sum_lo = sums.tile([P, CHUNK], F32)
-                if o % 8 == 3:
-                    nc.scalar.activation(
-                        out=sum_lo[:], in_=g_lo[:], func=ACT.Identity,
-                        bias=c_cols[:, 0, col : col + 1], scale=1.0,
+            def log_piece(part, a):
+                x_codes, x_scales = codes[chunk * PARTS + part]
+                grown = tokens.tile([P, X_PART], F32)
+                for first in range(0, X_PART, BANK):
+                    z = psum_small.tile([P, BANK], F32, tag="z")
+                    nc.tensor.matmul_mx(
+                        out=z[:],
+                        lhsT=w_codes[:, j, a, :].bitcast(FP8X4),
+                        lhsT_scale=w_scales[:, j, a, :],
+                        rhs=x_codes[:, first : first + BANK].bitcast(FP8X4),
+                        rhs_scale=x_scales[:, first : first + BANK],
+                        start=True,
+                        stop=True,
                     )
+                    nc.vector.tensor_scalar(
+                        out=grown[:, first : first + BANK], in0=z[:], scalar1=0.0, scalar2=1.0,
+                        op0=ALU.max, op1=ALU.add,
+                    )
+                cols = slice(part * X_PART, (part + 1) * X_PART)
+                if a == 0:
+                    nc.scalar.activation(out=g_lo[:, cols], in_=grown[:], func=ACT.Ln)
                 else:
-                    nc.gpsimd.tensor_scalar(
-                        out=sum_lo[:], in0=g_lo[:], scalar1=c_cols[:, 0, col : col + 1],
-                        scalar2=1.0, op0=ALU.add, op1=ALU.mult,
-                    )
-                whole = o % 16 == 15
-                if whole:
-                    nc.gpsimd.tensor_tensor(
-                        out=excess[:], in0=excess[:], in1=sum_lo[:], op=ALU.add
-                    )
-                for b0 in range(0, BLOCKS, BANK_BLOCKS):
-                    pair_max = psum_sums.tile([P, BANK_BLOCKS, P], F32)
-                    for b in range(BANK_BLOCKS):
-                        cols = slice((b0 + b) * P, (b0 + b + 1) * P)
-                        if not whole:
-                            nc.tensor.matmul(
-                                out=pair_max[:, b, :], lhsT=sum_lo[:, cols], rhs=ident[:],
-                                start=True, stop=False, is_transpose=True,
-                            )
-                        nc.tensor.matmul(
-                            out=pair_max[:, b, :], lhsT=excess[:, cols], rhs=ident[:],
-                            start=whole, stop=True, is_transpose=True,
-                        )
-                    nc.vector.tensor_reduce(
-                        out=y[:, b0 : b0 + BANK_BLOCKS, :, o],
-                        in_=pair_max[:].rearrange("p b (h i) -> p b h i", h=HEADS),
-                        axis=X_AXIS,
-                        op=ALU.max,
+                    nc.scalar.activation(out=g_hi[:, cols], in_=grown[:], func=ACT.Ln)
+                    nc.vector.tensor_sub(
+                        out=g_step[:, cols], in0=g_hi[:, cols], in1=g_lo[:, cols]
                     )
 
-        def store(chunk, j, y):
-            for b in range(BLOCKS):
+            steps = [
+                lambda part=part, a=a: log_piece(part, a)
+                for part in range(PARTS)
+                for a in range(2)
+            ]
+            return g_lo, g_step, steps
+
+        def tropical(g_lo, g_step, j, o, y, blocks):
+            col = j * DK + o
+            cols = slice(blocks.start * P, blocks.stop * P)
+            width = len(blocks) * P
+            excess = sums.tile([P, width], F32)
+            nc.scalar.activation(
+                out=excess[:], in_=g_step[:, cols], func=ACT.Relu,
+                bias=c_cols[:, 1, col : col + 1], scale=1.0,
+            )
+            sum_lo = sums.tile([P, width], F32)
+            if o % SCALAR_ADDS_EVERY == 1:
+                nc.scalar.activation(
+                    out=sum_lo[:], in_=g_lo[:, cols], func=ACT.Identity,
+                    bias=c_cols[:, 0, col : col + 1], scale=1.0,
+                )
+            else:
+                nc.gpsimd.tensor_scalar(
+                    out=sum_lo[:], in0=g_lo[:, cols], scalar1=c_cols[:, 0, col : col + 1],
+                    scalar2=1.0, op0=ALU.add, op1=ALU.mult,
+                )
+            whole = o % WHOLE_SUM_EVERY == 5
+            if whole:
+                nc.gpsimd.tensor_tensor(out=excess[:], in0=excess[:], in1=sum_lo[:], op=ALU.add)
+            for b0 in range(0, len(blocks), BANK_BLOCKS):
+                pair_max = psum_sums.tile([P, BANK_BLOCKS, P], F32)
+                for b in range(BANK_BLOCKS):
+                    block_cols = slice((b0 + b) * P, (b0 + b + 1) * P)
+                    if not whole:
+                        nc.tensor.matmul(
+                            out=pair_max[:, b, :], lhsT=sum_lo[:, block_cols], rhs=ident[:],
+                            start=True, stop=False, is_transpose=True,
+                        )
+                    nc.tensor.matmul(
+                        out=pair_max[:, b, :], lhsT=excess[:, block_cols], rhs=ident[:],
+                        start=whole, stop=True, is_transpose=True,
+                    )
+                nc.vector.tensor_reduce(
+                    out=y[:, blocks.start + b0 : blocks.start + b0 + BANK_BLOCKS, :, o],
+                    in_=pair_max[:].rearrange("p b (h i) -> p b h i", h=HEADS),
+                    axis=X_AXIS,
+                    op=ALU.max,
+                )
+
+        def store(chunk, j, y, blocks):
+            for b in blocks:
                 first = chunk * CHUNK + b * P
                 batch, l0 = first // BATCH_LEN, first % BATCH_LEN
                 nc.sync.dma_start(
@@ -244,36 +281,56 @@ def tile_tropicalattention_pa_t_kernel(
                     in_=y[:, b, :, :],
                 )
 
-        quarters = [range(q * DK // 4, (q + 1) * DK // 4) for q in range(4)]
-        next_codes = codes
-        g_lo = logs.tile([P, CHUNK], F32)
-        log_half(codes[0], codes[1], 0, 0, g_lo)
-        g_hi = tokens.tile([P, CHUNK], F32)
-        log_half(codes[0], codes[1], 0, 1, g_hi)
-        g_step = logs.tile([P, CHUNK], F32)
-        nc.vector.tensor_sub(out=g_step[:], in0=g_hi[:], in1=g_lo[:])
-        for stage in range(N_CHUNKS * PROJ):
-            chunk, j = divmod(stage, PROJ)
-            next_j = (j + 1) % PROJ
-            more = stage + 1 < N_CHUNKS * PROJ
-            if next_j == 0:
-                codes = next_codes
-            y = results.tile([P, BLOCKS, HEADS, DK], F32)
+        todo = []
+        taken = [0]
 
-            tropical(g_lo, g_step, j, quarters[0], y)
-            if more:
-                next_lo = logs.tile([P, CHUNK], F32, tag="g_lo")
-                log_half(codes[0], codes[1], next_j, 0, next_lo)
-            tropical(g_lo, g_step, j, quarters[1], y)
-            if more:
-                g_hi = tokens.tile([P, CHUNK], F32)
-                log_half(codes[0], codes[1], next_j, 1, g_hi)
-                next_step = logs.tile([P, CHUNK], F32, tag="g_step")
-                nc.vector.tensor_sub(out=next_step[:], in0=g_hi[:], in1=next_lo[:])
-            tropical(g_lo, g_step, j, quarters[2], y)
-            if j == 0 and chunk + 1 < N_CHUNKS:
-                next_codes = quantise_chunk(chunk + 1)
-            tropical(g_lo, g_step, j, quarters[3], y)
-            store(chunk, j, y)
-            if more:
+        def advance():
+            if taken[0] < len(todo):
+                todo[taken[0]]()
+                taken[0] += 1
+
+        def finish_steps():
+            while taken[0] < len(todo):
+                advance()
+
+        def sweep(g_lo, g_step, j, o_range, y, blocks):
+            for o in o_range:
+                tropical(g_lo, g_step, j, o, y, blocks)
+                if o % 2 == 1:
+                    advance()
+
+        all_blocks = range(BLOCKS)
+        halves = [range(0, BLOCKS // 2), range(BLOCKS // 2, BLOCKS)]
+        edge = DK // 4
+        stages = N_CHUNKS * PROJ
+
+        g_lo, g_step, own_steps = log_steps(0, 0)
+        own_steps[0]()
+        own_steps[1]()
+        todo.extend(x_steps(1))
+        todo.extend(own_steps[2:])
+        for stage in range(stages):
+            chunk, j = divmod(stage, PROJ)
+            y = results.tile([P, BLOCKS, HEADS, DK], F32)
+            start_o = 0
+            if stage == 0:
+                sweep(g_lo, g_step, j, range(edge), y, halves[0])
+                finish_steps()
+                start_o = edge
+            if stage + 1 < stages:
+                next_lo, next_step, next_steps = log_steps(*divmod(stage + 1, PROJ))
+                if len(codes) < TOKENS // X_PART:
+                    todo.extend(x_steps(len(codes)))
+                todo.extend(next_steps)
+            if stage == 0:
+                sweep(g_lo, g_step, j, range(edge), y, halves[1])
+            if stage + 1 < stages:
+                sweep(g_lo, g_step, j, range(start_o, DK), y, all_blocks)
+                finish_steps()
+                store(chunk, j, y, all_blocks)
                 g_lo, g_step = next_lo, next_step
+            else:
+                sweep(g_lo, g_step, j, range(start_o, DK - edge), y, all_blocks)
+                for half in halves:
+                    sweep(g_lo, g_step, j, range(DK - edge, DK), y, half)
+                    store(chunk, j, y, half)

@@ -25,11 +25,11 @@ CHUNK = 2048
 BLOCKS = CHUNK // P
 BANK_BLOCKS = BANK // P
 N_CHUNKS = TOKENS // CHUNK
-X_PART = 1024
+X_PART = 512
 X_BLOCKS = X_PART // P
 PARTS = CHUNK // X_PART
-SCALAR_ADDS_EVERY = 6
-WHOLE_SUM_EVERY = 11
+SCALAR_ADDS_EVERY = 7
+WHOLE_SUM_EVERY = 13
 LOG_LIMIT = 89.0
 
 FLOPS = 2 * TOKENS * D * PROJ * E + 2 * TOKENS * PROJ * E * DK
@@ -61,10 +61,10 @@ def tile_tropicalattention_pa_t_kernel(
         tc.tile_pool(name="tokens", bufs=2) as tokens,
         tc.tile_pool(name="coded", bufs=TOKENS // X_PART) as coded,
         tc.tile_pool(name="logs", bufs=2) as logs,
-        tc.tile_pool(name="sums", bufs=4) as sums,
+        tc.tile_pool(name="sums", bufs=6) as sums,
         tc.tile_pool(name="results", bufs=2) as results,
         tc.psum_pool(name="psum_small", bufs=2) as psum_small,
-        tc.psum_pool(name="psum_sums", bufs=4) as psum_sums,
+        tc.psum_pool(name="psum_sums", bufs=6) as psum_sums,
     ):
         ident = const.tile([P, P], F32)
         make_identity(nc, ident[:])
@@ -86,7 +86,7 @@ def tile_tropicalattention_pa_t_kernel(
             codes.append((x_codes, x_scales))
 
             def turn_two_blocks(two):
-                turned = psum_small.tile([P, 2, 2, P], F32, tag="turned")
+                turned = psum_small.tile([P, 2, 2, P], F32, tag="small")
                 for b in range(2):
                     x_words = x_sb[:, 2 * two + b, :].bitcast(F32)
                     for u in range(2):
@@ -177,7 +177,7 @@ def tile_tropicalattention_pa_t_kernel(
         nc.vector.tensor_sub(
             out=c_rows[:, 1, :, :, :], in0=c[:, :, :, HALF:DK], in1=c[:, :, :, 0:HALF]
         )
-        c_turned = psum_small.tile([P, 2, 2, P], F32, tag="turned")
+        c_turned = psum_small.tile([P, 2, 2, P], F32, tag="small")
         for kind in range(2):
             for square in range(2):
                 nc.tensor.transpose(
@@ -193,39 +193,35 @@ def tile_tropicalattention_pa_t_kernel(
             g_step = logs.tile([P, CHUNK], F32)
             g_hi = tokens.tile([P, CHUNK], F32)
 
-            def log_piece(part, a):
+            def log_part(part):
                 x_codes, x_scales = codes[chunk * PARTS + part]
-                grown = tokens.tile([P, X_PART], F32)
-                for first in range(0, X_PART, BANK):
-                    z = psum_small.tile([P, BANK], F32, tag="z")
+                cols = slice(part * X_PART, (part + 1) * X_PART)
+                grown = tokens.tile([P, 2, X_PART], F32)
+                for a in range(2):
+                    z = psum_small.tile([P, BANK], F32, tag="small")
                     nc.tensor.matmul_mx(
                         out=z[:],
                         lhsT=w_codes[:, j, a, :].bitcast(FP8X4),
                         lhsT_scale=w_scales[:, j, a, :],
-                        rhs=x_codes[:, first : first + BANK].bitcast(FP8X4),
-                        rhs_scale=x_scales[:, first : first + BANK],
+                        rhs=x_codes[:].bitcast(FP8X4),
+                        rhs_scale=x_scales[:],
                         start=True,
                         stop=True,
                     )
                     nc.vector.tensor_scalar(
-                        out=grown[:, first : first + BANK], in0=z[:], scalar1=0.0, scalar2=1.0,
+                        out=grown[:, a, :], in0=z[:], scalar1=0.0, scalar2=1.0,
                         op0=ALU.max, op1=ALU.add,
                     )
-                cols = slice(part * X_PART, (part + 1) * X_PART)
-                if a == 0:
-                    nc.scalar.activation(out=g_lo[:, cols], in_=grown[:], func=ACT.Ln)
-                else:
-                    nc.scalar.activation(out=g_hi[:, cols], in_=grown[:], func=ACT.Ln)
-                    nc.vector.tensor_sub(
-                        out=g_step[:, cols], in0=g_hi[:, cols], in1=g_lo[:, cols]
-                    )
+                nc.scalar.activation(out=g_lo[:, cols], in_=grown[:, 0, :], func=ACT.Ln)
+                nc.scalar.activation(out=g_hi[:, cols], in_=grown[:, 1, :], func=ACT.Ln)
 
-            steps = [
-                lambda part=part, a=a: log_piece(part, a)
-                for part in range(PARTS)
-                for a in range(2)
-            ]
-            return g_lo, g_step, steps
+            def subtract(half):
+                cols = slice(half * CHUNK // 2, (half + 1) * CHUNK // 2)
+                nc.vector.tensor_sub(out=g_step[:, cols], in0=g_hi[:, cols], in1=g_lo[:, cols])
+
+            log_parts = [lambda part=part: log_part(part) for part in range(PARTS)]
+            subtractions = [lambda half=half: subtract(half) for half in range(2)]
+            return g_lo, g_step, log_parts, subtractions
 
         def tropical(g_lo, g_step, j, o, y, blocks):
             col = j * DK + o
@@ -237,7 +233,7 @@ def tile_tropicalattention_pa_t_kernel(
                 bias=c_cols[:, 1, col : col + 1], scale=1.0,
             )
             sum_lo = sums.tile([P, width], F32)
-            if o % SCALAR_ADDS_EVERY == 1:
+            if o % SCALAR_ADDS_EVERY == 3:
                 nc.scalar.activation(
                     out=sum_lo[:], in_=g_lo[:, cols], func=ACT.Identity,
                     bias=c_cols[:, 0, col : col + 1], scale=1.0,
@@ -247,7 +243,7 @@ def tile_tropicalattention_pa_t_kernel(
                     out=sum_lo[:], in0=g_lo[:, cols], scalar1=c_cols[:, 0, col : col + 1],
                     scalar2=1.0, op0=ALU.add, op1=ALU.mult,
                 )
-            whole = o % WHOLE_SUM_EVERY == 5
+            whole = o % WHOLE_SUM_EVERY == 6
             if whole:
                 nc.gpsimd.tensor_tensor(out=excess[:], in0=excess[:], in1=sum_lo[:], op=ALU.add)
             for b0 in range(0, len(blocks), BANK_BLOCKS):
@@ -296,41 +292,53 @@ def tile_tropicalattention_pa_t_kernel(
         def sweep(g_lo, g_step, j, o_range, y, blocks):
             for o in o_range:
                 tropical(g_lo, g_step, j, o, y, blocks)
-                if o % 2 == 1:
-                    advance()
+                advance()
+
+        def pause(steps):
+            return [lambda: None for step in range(steps)]
 
         all_blocks = range(BLOCKS)
         halves = [range(0, BLOCKS // 2), range(BLOCKS // 2, BLOCKS)]
+        half_parts = PARTS // 2
         edge = DK // 4
         stages = N_CHUNKS * PROJ
 
-        g_lo, g_step, own_steps = log_steps(0, 0)
-        own_steps[0]()
-        own_steps[1]()
-        todo.extend(x_steps(1))
-        todo.extend(own_steps[2:])
-        for stage in range(stages):
-            chunk, j = divmod(stage, PROJ)
-            y = results.tile([P, BLOCKS, HEADS, DK], F32)
-            start_o = 0
-            if stage == 0:
-                sweep(g_lo, g_step, j, range(edge), y, halves[0])
-                finish_steps()
-                start_o = edge
-            if stage + 1 < stages:
-                next_lo, next_step, next_steps = log_steps(*divmod(stage + 1, PROJ))
-                if len(codes) < TOKENS // X_PART:
-                    todo.extend(x_steps(len(codes)))
-                todo.extend(next_steps)
-            if stage == 0:
-                sweep(g_lo, g_step, j, range(edge), y, halves[1])
-            if stage + 1 < stages:
-                sweep(g_lo, g_step, j, range(start_o, DK), y, all_blocks)
-                finish_steps()
-                store(chunk, j, y, all_blocks)
-                g_lo, g_step = next_lo, next_step
-            else:
-                sweep(g_lo, g_step, j, range(start_o, DK - edge), y, all_blocks)
-                for half in halves:
-                    sweep(g_lo, g_step, j, range(DK - edge, DK), y, half)
-                    store(chunk, j, y, half)
+        for part in range(1, half_parts):
+            for step in x_steps(part):
+                step()
+        g_lo, g_step, log_parts, subtractions = log_steps(0, 0)
+        for step in log_parts[:half_parts]:
+            step()
+        subtractions[0]()
+        with tc.manual_schedule(engines={mybir.EngineType.DVE}):
+            for part in range(half_parts, PARTS):
+                todo.extend(x_steps(part))
+            todo.extend(log_parts[half_parts:] + pause(3) + subtractions[1:])
+            for stage in range(stages):
+                chunk, j = divmod(stage, PROJ)
+                y = results.tile([P, BLOCKS, HEADS, DK], F32)
+                start_o = 0
+                if stage == 0:
+                    sweep(g_lo, g_step, j, range(edge), y, halves[0])
+                    finish_steps()
+                    start_o = edge
+                if stage + 1 < stages:
+                    next_lo, next_step, log_parts, subtractions = log_steps(
+                        *divmod(stage + 1, PROJ)
+                    )
+                    for part in range(half_parts):
+                        if len(codes) < TOKENS // X_PART:
+                            todo.extend(x_steps(len(codes)))
+                    todo.extend(log_parts + pause(6) + subtractions)
+                if stage == 0:
+                    sweep(g_lo, g_step, j, range(edge), y, halves[1])
+                if stage + 1 < stages:
+                    sweep(g_lo, g_step, j, range(start_o, DK), y, all_blocks)
+                    finish_steps()
+                    store(chunk, j, y, all_blocks)
+                    g_lo, g_step = next_lo, next_step
+                else:
+                    sweep(g_lo, g_step, j, range(start_o, DK - edge), y, all_blocks)
+                    for half in halves:
+                        sweep(g_lo, g_step, j, range(DK - edge, DK), y, half)
+                        store(chunk, j, y, half)

@@ -28,8 +28,8 @@ N_CHUNKS = TOKENS // CHUNK
 X_PART = 512
 X_BLOCKS = X_PART // P
 PARTS = CHUNK // X_PART
-SCALAR_ADDS_EVERY = 7
-WHOLE_SUM_EVERY = 13
+SCALAR_ADDS_EVERY = 8
+WHOLE_SUM_EVERY = 16
 LOG_LIMIT = 89.0
 
 FLOPS = 2 * TOKENS * D * PROJ * E + 2 * TOKENS * PROJ * E * DK

@@ -11,6 +11,7 @@ ACT = mybir.ActivationFunctionType
 ALU = mybir.AluOpType
 X_AXIS = mybir.AxisListType.X
 
+
 P = 128
 TOKENS = 16 * 256
 BATCH_LEN = 256
@@ -18,19 +19,27 @@ D = 512
 HEADS = 4
 DK = 64
 HALF = DK // 2
+QUARTER = DK // 4
 E = HEADS * DK
 PROJ = 3
 BANK = 512
-CHUNK = 2048
-BLOCKS = CHUNK // P
 BANK_BLOCKS = BANK // P
-N_CHUNKS = TOKENS // CHUNK
-X_PART = 512
-X_BLOCKS = X_PART // P
-PARTS = CHUNK // X_PART
-SCALAR_ADDS_EVERY = 8
-WHOLE_SUM_EVERY = 16
+PART = 512
+PARTS = TOKENS // PART
+PART_BLOCKS = PART // P
+RELU_BLOCKS = 8
 LOG_LIMIT = 89.0
+
+STAGES = [
+    (0, [0, 1, 2, 3]),
+    (1, [0, 1, 2, 3]),
+    (2, [0, 1, 2, 3]),
+    (0, [4, 5, 6]),
+    (1, [4, 5, 6]),
+    (2, [4, 5]),
+]
+QUAD_PARTS = [[7], [6, 7]]
+QUAD_EVERY = 9
 
 FLOPS = 2 * TOKENS * D * PROJ * E + 2 * TOKENS * PROJ * E * DK
 
@@ -59,34 +68,36 @@ def tile_tropicalattention_pa_t_kernel(
     with (
         tc.tile_pool(name="const", bufs=1) as const,
         tc.tile_pool(name="tokens", bufs=2) as tokens,
-        tc.tile_pool(name="coded", bufs=TOKENS // X_PART) as coded,
+        tc.tile_pool(name="coded", bufs=PARTS) as coded,
         tc.tile_pool(name="logs", bufs=2) as logs,
-        tc.tile_pool(name="sums", bufs=6) as sums,
+        tc.tile_pool(name="lows", bufs=4) as lows,
+        tc.tile_pool(name="relus", bufs=6) as relus,
         tc.tile_pool(name="results", bufs=2) as results,
-        tc.psum_pool(name="psum_small", bufs=2) as psum_small,
-        tc.psum_pool(name="psum_sums", bufs=6) as psum_sums,
+        tc.tile_pool(name="quad", bufs=2) as quad,
+        tc.tile_pool(name="quad_units", bufs=4) as quad_units,
+        tc.tile_pool(name="quad_results", bufs=1) as quad_results,
+        tc.psum_pool(name="banks", bufs=6) as banks,
+        tc.psum_pool(name="kept_banks", bufs=1) as kept_banks,
     ):
         ident = const.tile([P, P], F32)
         make_identity(nc, ident[:])
 
-        codes = []
+        codes = {}
 
         def x_steps(part):
-            x_sb = tokens.tile([P, X_BLOCKS, D], BF16)
+            x_sb = tokens.tile([P, PART_BLOCKS, D], BF16)
             nc.sync.dma_start(
                 out=x_sb[:],
-                in_=x_rows[part * X_PART : (part + 1) * X_PART, :].rearrange(
-                    "(b p) k -> p b k", p=P
-                ),
+                in_=x_rows[part * PART : (part + 1) * PART, :].rearrange("(b p) k -> p b k", p=P),
             )
-            grouped = tokens.tile([P, X_PART, 4], BF16, align_bytes=64)
+            grouped = tokens.tile([P, PART, 4], BF16, align_bytes=64)
             grouped_words = grouped[:].bitcast(F32)
-            x_codes = coded.tile([P, X_PART], U32, align_bytes=64)
-            x_scales = coded.tile([P, X_PART], U8, align_bytes=64)
-            codes.append((x_codes, x_scales))
+            x_codes = coded.tile([P, PART], U32, align_bytes=64)
+            x_scales = coded.tile([P, PART], U8, align_bytes=64)
+            codes[part] = (x_codes, x_scales)
 
             def turn_two_blocks(two):
-                turned = psum_small.tile([P, 2, 2, P], F32, tag="small")
+                turned = banks.tile([P, 2, 2, P], F32, tag="bank")
                 for b in range(2):
                     x_words = x_sb[:, 2 * two + b, :].bitcast(F32)
                     for u in range(2):
@@ -107,7 +118,7 @@ def tile_tropicalattention_pa_t_kernel(
                     in_=grouped[:].rearrange("p r t -> p (r t)"),
                 )
 
-            return [lambda two=two: turn_two_blocks(two) for two in range(X_BLOCKS // 2)] + [
+            return [lambda two=two: turn_two_blocks(two) for two in range(PART_BLOCKS // 2)] + [
                 quantise
             ]
 
@@ -177,7 +188,7 @@ def tile_tropicalattention_pa_t_kernel(
         nc.vector.tensor_sub(
             out=c_rows[:, 1, :, :, :], in0=c[:, :, :, HALF:DK], in1=c[:, :, :, 0:HALF]
         )
-        c_turned = psum_small.tile([P, 2, 2, P], F32, tag="small")
+        c_turned = banks.tile([P, 2, 2, P], F32, tag="bank")
         for kind in range(2):
             for square in range(2):
                 nc.tensor.transpose(
@@ -188,94 +199,276 @@ def tile_tropicalattention_pa_t_kernel(
         c_cols = const.tile([P, 2, 2 * P], F32)
         nc.vector.tensor_copy(out=c_cols[:], in_=c_turned[:].rearrange("p k s o -> p k (s o)"))
 
-        def log_steps(chunk, j):
-            g_lo = logs.tile([P, CHUNK], F32)
-            g_step = logs.tile([P, CHUNK], F32)
-            g_hi = tokens.tile([P, CHUNK], F32)
+        quad_codes = const.tile([P, 2, 4, P], U32, align_bytes=64)
+        quad_scales = const.tile([P, 2, 4, P], U8, align_bytes=64)
+        quad_rows = const.tile([P, 2, 4, 2, HEADS, QUARTER], F32)
+        quad_cols = const.tile([P, 2, 4, DK], F32)
 
-            def log_part(part):
-                x_codes, x_scales = codes[chunk * PARTS + part]
-                cols = slice(part * X_PART, (part + 1) * X_PART)
-                grown = tokens.tile([P, 2, X_PART], F32)
-                for a in range(2):
-                    z = psum_small.tile([P, BANK], F32, tag="small")
-                    nc.tensor.matmul_mx(
-                        out=z[:],
-                        lhsT=w_codes[:, j, a, :].bitcast(FP8X4),
-                        lhsT_scale=w_scales[:, j, a, :],
-                        rhs=x_codes[:].bitcast(FP8X4),
-                        rhs_scale=x_scales[:],
-                        start=True,
-                        stop=True,
+        def quad_weights(s, f):
+            a, i0 = f // 2, (f % 2) * QUARTER
+            codes_from = w_codes[:].bitcast(I32).rearrange("p j a (h i) -> p j a h i", h=HEADS)
+            scales_from = w_scales[:].bitcast(I32).rearrange("p j a (h w) -> p j a h w", h=HEADS)
+            codes_to = quad_codes[:, s, f, :].bitcast(I32).rearrange(
+                "p (g h i) -> p g h i", g=2, h=HEADS
+            )
+            scales_to = quad_scales[:, s, f, :].bitcast(I32).rearrange(
+                "p (g h w) -> p g h w", g=2, h=HEADS
+            )
+            for g in range(2):
+                j = 2 if s == 1 else g
+                nc.gpsimd.tensor_copy(
+                    out=codes_to[:, g, :, :], in_=codes_from[:, j, a, :, i0 : i0 + QUARTER]
+                )
+                nc.gpsimd.tensor_copy(
+                    out=scales_to[:, g, :, :],
+                    in_=scales_from[:, j, a, :, i0 // 4 : (i0 + QUARTER) // 4],
+                )
+
+        def quad_constants(g):
+            for s in range(2):
+                nc.vector.tensor_copy(out=quad_rows[:, s, 0, g, :, :], in_=c[:, s, :, 0:QUARTER])
+            for f in range(1, 4):
+                nc.vector.tensor_sub(
+                    out=quad_rows[:, :, f, g, :, :],
+                    in0=c[:, :, :, f * QUARTER : (f + 1) * QUARTER],
+                    in1=c[:, :, :, 0:QUARTER],
+                )
+
+        def quad_turn_constants(s):
+            turned = banks.tile([P, 4, P], F32, tag="bank")
+            for kind in range(4):
+                nc.tensor.transpose(
+                    turned[:, kind, :],
+                    quad_rows[:, s, kind, :, :, :].rearrange("p g h i -> p (g h i)"),
+                    ident[:],
+                )
+            for g in range(2):
+                rows = slice(g * DK, (g + 1) * DK)
+                nc.vector.tensor_copy(out=quad_cols[rows, s, :, :], in_=turned[rows, :, rows])
+
+        def mx_pass(part, lhs_codes, lhs_scales):
+            x_codes, x_scales = codes[part]
+            z = banks.tile([P, BANK], F32, tag="bank")
+            nc.tensor.matmul_mx(
+                out=z[:],
+                lhsT=lhs_codes.bitcast(FP8X4),
+                lhsT_scale=lhs_scales,
+                rhs=x_codes[:].bitcast(FP8X4),
+                rhs_scale=x_scales[:],
+                start=True,
+                stop=True,
+            )
+            return z
+
+        def relu_plus_one(out, z):
+            nc.vector.tensor_scalar(
+                out=out, in0=z, scalar1=0.0, scalar2=1.0, op0=ALU.max, op1=ALU.add
+            )
+
+        def log_steps(j, parts):
+            g_lo = logs.tile([P, len(parts) * PART], F32)
+            g_step = logs.tile([P, len(parts) * PART], F32)
+
+            def log_half(n, a):
+                cols = slice(n * PART, (n + 1) * PART)
+                grown = tokens.tile([P, PART], F32)
+                z = mx_pass(parts[n], w_codes[:, j, a, :], w_scales[:, j, a, :])
+                relu_plus_one(grown[:], z[:])
+                if a == 0:
+                    nc.scalar.activation(out=g_lo[:, cols], in_=grown[:], func=ACT.Ln)
+                else:
+                    g_hi = tokens.tile([P, PART], F32)
+                    nc.scalar.activation(out=g_hi[:], in_=grown[:], func=ACT.Ln)
+                    nc.gpsimd.tensor_tensor(
+                        out=g_step[:, cols], in0=g_hi[:], in1=g_lo[:, cols], op=ALU.subtract
                     )
-                    nc.vector.tensor_scalar(
-                        out=grown[:, a, :], in0=z[:], scalar1=0.0, scalar2=1.0,
-                        op0=ALU.max, op1=ALU.add,
-                    )
-                nc.scalar.activation(out=g_lo[:, cols], in_=grown[:, 0, :], func=ACT.Ln)
-                nc.scalar.activation(out=g_hi[:, cols], in_=grown[:, 1, :], func=ACT.Ln)
 
-            def subtract(half):
-                cols = slice(half * CHUNK // 2, (half + 1) * CHUNK // 2)
-                nc.vector.tensor_sub(out=g_step[:, cols], in0=g_hi[:, cols], in1=g_lo[:, cols])
+            steps = [
+                lambda n=n, a=a: log_half(n, a) for n in range(len(parts)) for a in range(2)
+            ]
+            return g_lo, g_step, steps
 
-            log_parts = [lambda part=part: log_part(part) for part in range(PARTS)]
-            subtractions = [lambda half=half: subtract(half) for half in range(2)]
-            return g_lo, g_step, log_parts, subtractions
+        banks_done = [0]
+        events = {}
+
+        def tick():
+            banks_done[0] += 1
+            for work in events.get(banks_done[0], []):
+                work()
 
         def tropical(g_lo, g_step, j, o, y, blocks):
             col = j * DK + o
-            cols = slice(blocks.start * P, blocks.stop * P)
-            width = len(blocks) * P
-            excess = sums.tile([P, width], F32)
-            nc.scalar.activation(
-                out=excess[:], in_=g_step[:, cols], func=ACT.Relu,
-                bias=c_cols[:, 1, col : col + 1], scale=1.0,
+            sum_lo = lows.tile([P, len(blocks) * P], F32)
+            nc.gpsimd.tensor_scalar(
+                out=sum_lo[:], in0=g_lo[:, blocks.start * P : blocks.stop * P],
+                scalar1=c_cols[:, 0, col : col + 1],
+                scalar2=1.0, op0=ALU.add, op1=ALU.mult,
             )
-            sum_lo = sums.tile([P, width], F32)
-            if o % SCALAR_ADDS_EVERY == 3:
+            for r0 in range(0, len(blocks), RELU_BLOCKS):
+                width = min(RELU_BLOCKS, len(blocks) - r0)
+                first = blocks.start + r0
+                excess = relus.tile([P, width * P], F32)
                 nc.scalar.activation(
-                    out=sum_lo[:], in_=g_lo[:, cols], func=ACT.Identity,
-                    bias=c_cols[:, 0, col : col + 1], scale=1.0,
+                    out=excess[:], in_=g_step[:, first * P : (first + width) * P], func=ACT.Relu,
+                    bias=c_cols[:, 1, col : col + 1], scale=1.0,
                 )
-            else:
-                nc.gpsimd.tensor_scalar(
-                    out=sum_lo[:], in0=g_lo[:, cols], scalar1=c_cols[:, 0, col : col + 1],
-                    scalar2=1.0, op0=ALU.add, op1=ALU.mult,
-                )
-            whole = o % WHOLE_SUM_EVERY == 6
-            if whole:
-                nc.gpsimd.tensor_tensor(out=excess[:], in0=excess[:], in1=sum_lo[:], op=ALU.add)
-            for b0 in range(0, len(blocks), BANK_BLOCKS):
-                pair_max = psum_sums.tile([P, BANK_BLOCKS, P], F32)
-                for b in range(BANK_BLOCKS):
-                    block_cols = slice((b0 + b) * P, (b0 + b + 1) * P)
-                    if not whole:
+                for b0 in range(0, width, BANK_BLOCKS):
+                    pair_max = banks.tile([P, BANK_BLOCKS, P], F32, tag="bank")
+                    for b in range(BANK_BLOCKS):
                         nc.tensor.matmul(
-                            out=pair_max[:, b, :], lhsT=sum_lo[:, block_cols], rhs=ident[:],
-                            start=True, stop=False, is_transpose=True,
+                            out=pair_max[:, b, :],
+                            lhsT=sum_lo[:, (r0 + b0 + b) * P : (r0 + b0 + b + 1) * P],
+                            rhs=ident[:], start=True, stop=False, is_transpose=True,
                         )
+                        nc.tensor.matmul(
+                            out=pair_max[:, b, :],
+                            lhsT=excess[:, (b0 + b) * P : (b0 + b + 1) * P],
+                            rhs=ident[:], start=False, stop=True, is_transpose=True,
+                        )
+                    nc.vector.tensor_reduce(
+                        out=y[:, first + b0 : first + b0 + BANK_BLOCKS, :, o],
+                        in_=pair_max[:].rearrange("p b (h i) -> p b h i", h=HEADS),
+                        axis=X_AXIS,
+                        op=ALU.max,
+                    )
+                    tick()
+
+        def store(j, parts, y, blocks):
+            for b in blocks:
+                first = parts[b // PART_BLOCKS] * PART + (b % PART_BLOCKS) * P
+                store_block(j, first, y[:, b, :, :])
+
+        def store_block(j, first, rows):
+            batch, l0 = first // BATCH_LEN, first % BATCH_LEN
+            nc.sync.dma_start(
+                out=outs[j][batch * HEADS : (batch + 1) * HEADS, l0 : l0 + P, :].rearrange(
+                    "h l o -> l h o"
+                ),
+                in_=rows,
+            )
+
+        def pause(steps):
+            return [lambda: None for step in range(steps)]
+
+        def quad_steps(s):
+            stage = {}
+            base = quad.tile([P, PART], F32)
+            spread = quad.tile([P, PART], F32)
+            kept_rows = {}
+            grown_of = {}
+
+            def log_quarter(f, g):
+                parts = QUAD_PARTS[s]
+                rows = slice(0, P) if len(parts) == 1 else slice(g * DK, (g + 1) * DK)
+                if g == 0:
+                    grown = tokens.tile([P, PART], F32)
+                    grown_of[f] = grown
+                z = mx_pass(parts[g], quad_codes[:, s, f, :], quad_scales[:, s, f, :])
+                relu_plus_one(grown_of[f][rows, :], z[rows, :])
+                if g < len(parts) - 1:
+                    return
+                if f == 0:
+                    nc.scalar.activation(out=base[:], in_=grown_of[f][:], func=ACT.Ln)
+                    return
+                g_hi = tokens.tile([P, PART], F32)
+                nc.scalar.activation(out=g_hi[:], in_=grown_of[f][:], func=ACT.Ln)
+                if f == 1:
+                    step = spread
+                else:
+                    step = quad.tile([P, PART], F32)
+                    kept_rows[f] = step
+                nc.gpsimd.tensor_tensor(out=step[:], in0=g_hi[:], in1=base[:], op=ALU.subtract)
+
+            def turn_step(f):
+                turned = banks.tile([P, PART_BLOCKS, P], F32, tag="bank")
+                for b in range(PART_BLOCKS):
+                    nc.tensor.transpose(
+                        turned[:, b, :], kept_rows[f][:, b * P : (b + 1) * P], ident[:]
+                    )
+                by_token = quad.tile([P, PART_BLOCKS, P], F32)
+                nc.vector.tensor_copy(out=by_token[:], in_=turned[:])
+                kept_rows[f] = by_token
+
+            def keep():
+                for f in (2, 3):
+                    kept = kept_banks.tile([P, PART], F32, tag="kept%d" % f)
+                    for b in range(PART_BLOCKS):
+                        nc.tensor.transpose(
+                            kept[:, b * P : (b + 1) * P], kept_rows[f][:, b, :], ident[:]
+                        )
+                    stage[f] = kept
+
+            stage["base"] = base
+            stage["spread"] = spread
+            passes = [(f, g) for f in range(4) for g in range(len(QUAD_PARTS[s]))]
+            logs_first = [lambda f=f, g=g: log_quarter(f, g) for f, g in passes]
+            turns = [lambda f=f: turn_step(f) for f in (2, 3)]
+            return logs_first, turns, keep, stage
+
+        def quad_unit(s, stage, o):
+            tiles = {}
+
+            def feed():
+                lead = quad_units.tile([P, PART], F32)
+                nc.scalar.activation(
+                    out=lead[:], in_=stage["spread"][:], func=ACT.Relu,
+                    bias=quad_cols[:, s, 1, o : o + 1], scale=1.0,
+                )
+                first = quad_units.tile([P, PART], F32)
+                nc.scalar.activation(
+                    out=first[:], in_=stage["base"][:], func=ACT.Identity,
+                    bias=quad_cols[:, s, 0, o : o + 1], scale=1.0,
+                )
+                tiles["lead"], tiles["first"] = lead, first
+
+            def grow(f):
+                lead = tiles["lead"]
+                nc.vector.scalar_tensor_tensor(
+                    out=lead[:], in0=stage[f][:], scalar=quad_cols[:, s, f, o : o + 1],
+                    in1=lead[:], op0=ALU.add, op1=ALU.max,
+                )
+
+            def finish():
+                if o == 0:
+                    y = quad_results.tile([P, PART_BLOCKS, 2, HEADS, DK], F32)
+                    stage["y"] = y
+                quad_max = banks.tile([P, PART_BLOCKS, P], F32, tag="bank")
+                for b in range(PART_BLOCKS):
+                    cols = slice(b * P, (b + 1) * P)
                     nc.tensor.matmul(
-                        out=pair_max[:, b, :], lhsT=excess[:, block_cols], rhs=ident[:],
-                        start=whole, stop=True, is_transpose=True,
+                        out=quad_max[:, b, :], lhsT=tiles["first"][:, cols], rhs=ident[:],
+                        start=True, stop=False, is_transpose=True,
+                    )
+                    nc.tensor.matmul(
+                        out=quad_max[:, b, :], lhsT=tiles["lead"][:, cols], rhs=ident[:],
+                        start=False, stop=True, is_transpose=True,
                     )
                 nc.vector.tensor_reduce(
-                    out=y[:, blocks.start + b0 : blocks.start + b0 + BANK_BLOCKS, :, o],
-                    in_=pair_max[:].rearrange("p b (h i) -> p b h i", h=HEADS),
+                    out=stage["y"][:].rearrange("p b g h o -> p b (g h) o")[:, :, :, o],
+                    in_=quad_max[:].rearrange("p b (c i) -> p b c i", i=QUARTER),
                     axis=X_AXIS,
                     op=ALU.max,
                 )
 
-        def store(chunk, j, y, blocks):
-            for b in blocks:
-                first = chunk * CHUNK + b * P
-                batch, l0 = first // BATCH_LEN, first % BATCH_LEN
-                nc.sync.dma_start(
-                    out=outs[j][batch * HEADS : (batch + 1) * HEADS, l0 : l0 + P, :].rearrange(
-                        "h l o -> l h o"
-                    ),
-                    in_=y[:, b, :, :],
-                )
+            return [feed, lambda: grow(2), lambda: grow(3), finish]
+
+        def quad_store(s, stage):
+            for b in range(PART_BLOCKS):
+                for g in range(2):
+                    j = 2 if s == 1 else g
+                    part = QUAD_PARTS[s][g if s == 1 else 0]
+                    store_block(j, part * PART + b * P, stage["y"][:, b, g, :, :])
+
+        def quad_run(s, stage, keep, first_bank):
+            work = [(first_bank, keep)]
+            for o in range(DK):
+                at = first_bank + o * QUAD_EVERY
+                feed, grow_2, grow_3, finish = quad_unit(s, stage, o)
+                work += [(at - 4, feed), (at + 3, grow_2), (at + 6, grow_3), (at + 13, finish)]
+            work += [(first_bank + DK * QUAD_EVERY + 5, lambda: quad_store(s, stage))]
+            for bank, piece in work:
+                events.setdefault(bank, []).append(piece)
+            return first_bank + (DK - 1) * QUAD_EVERY + 6
 
         todo = []
         taken = [0]
@@ -294,51 +487,63 @@ def tile_tropicalattention_pa_t_kernel(
                 tropical(g_lo, g_step, j, o, y, blocks)
                 advance()
 
-        def pause(steps):
-            return [lambda: None for step in range(steps)]
-
-        all_blocks = range(BLOCKS)
-        halves = [range(0, BLOCKS // 2), range(BLOCKS // 2, BLOCKS)]
-        half_parts = PARTS // 2
+        head_parts = 2
         edge = DK // 4
-        stages = N_CHUNKS * PROJ
+        last_edge = DK // 8
+        last_growth = [0]
 
-        for part in range(1, half_parts):
+        def start_quads(s, stage, keep):
+            first_bank = max(banks_done[0] + 5, last_growth[0] + 7)
+            last_growth[0] = quad_run(s, stage, keep, first_bank)
+
+        def prepare_quads(s, between):
+            logs_first, turns, keep, stage = quad_steps(s)
+            todo.extend(logs_first + between + turns)
+            todo.append(lambda: start_quads(s, stage, keep))
+
+        for part in range(1, head_parts):
             for step in x_steps(part):
                 step()
-        g_lo, g_step, log_parts, subtractions = log_steps(0, 0)
-        for step in log_parts[:half_parts]:
+        j, parts = STAGES[0]
+        g_lo, g_step, log_parts = log_steps(j, parts)
+        for step in log_parts[: 2 * head_parts]:
             step()
-        subtractions[0]()
         with tc.manual_schedule(engines={mybir.EngineType.DVE}):
-            for part in range(half_parts, PARTS):
+            for part in parts[head_parts:]:
                 todo.extend(x_steps(part))
-            todo.extend(log_parts[half_parts:] + pause(3) + subtractions[1:])
-            for stage in range(stages):
-                chunk, j = divmod(stage, PROJ)
-                y = results.tile([P, BLOCKS, HEADS, DK], F32)
+            todo.extend(log_parts[2 * head_parts :])
+            for stage, (j, parts) in enumerate(STAGES):
+                blocks = range(len(parts) * PART_BLOCKS)
+                halves = [range(0, len(blocks) // 2), range(len(blocks) // 2, len(blocks))]
+                y = results.tile([P, len(blocks), HEADS, DK], F32)
                 start_o = 0
                 if stage == 0:
                     sweep(g_lo, g_step, j, range(edge), y, halves[0])
                     finish_steps()
                     start_o = edge
-                if stage + 1 < stages:
-                    next_lo, next_step, log_parts, subtractions = log_steps(
-                        *divmod(stage + 1, PROJ)
-                    )
-                    for part in range(half_parts):
-                        if len(codes) < TOKENS // X_PART:
-                            todo.extend(x_steps(len(codes)))
-                    todo.extend(log_parts + pause(6) + subtractions)
+                    for f in range(4):
+                        quad_weights(0, f)
+                    todo.extend(x_steps(7))
+                    constants = [lambda g=g: quad_constants(g) for g in range(2)]
+                    constants += [lambda s=s: quad_turn_constants(s) for s in range(2)]
+                    prepare_quads(0, constants + pause(2))
+                if stage + 1 < len(STAGES):
+                    next_lo, next_step, log_parts = log_steps(*STAGES[stage + 1])
+                    todo.extend(log_parts)
+                if stage == 1:
+                    for part in (4, 5, 6):
+                        todo.extend(x_steps(part))
+                    todo.extend([lambda f=f: quad_weights(1, f) for f in range(4)])
+                    prepare_quads(1, pause(6))
                 if stage == 0:
                     sweep(g_lo, g_step, j, range(edge), y, halves[1])
-                if stage + 1 < stages:
-                    sweep(g_lo, g_step, j, range(start_o, DK), y, all_blocks)
+                if stage + 1 < len(STAGES):
+                    sweep(g_lo, g_step, j, range(start_o, DK), y, blocks)
                     finish_steps()
-                    store(chunk, j, y, all_blocks)
+                    store(j, parts, y, blocks)
                     g_lo, g_step = next_lo, next_step
                 else:
-                    sweep(g_lo, g_step, j, range(start_o, DK - edge), y, all_blocks)
+                    sweep(g_lo, g_step, j, range(start_o, DK - last_edge), y, blocks)
                     for half in halves:
-                        sweep(g_lo, g_step, j, range(DK - edge, DK), y, half)
-                        store(chunk, j, y, half)
+                        sweep(g_lo, g_step, j, range(DK - last_edge, DK), y, half)
+                        store(j, parts, y, half)

@@ -40,6 +40,7 @@ STAGES = [
 ]
 QUAD_PARTS = [[7], [6, 7]]
 QUAD_EVERY = 9
+GPSIMD_BASES, GPSIMD_BASES_OF = 3, 8
 
 FLOPS = 2 * TOKENS * D * PROJ * E + 2 * TOKENS * PROJ * E * DK
 
@@ -104,7 +105,8 @@ def tile_tropicalattention_pa_t_kernel(
                         nc.tensor.transpose(
                             turned[:, b, u, :], x_words[:, u : D // 2 : 2], ident[:]
                         )
-                nc.vector.tensor_copy(
+                copy = nc.vector.tensor_copy if part in STAGES[0][1] else nc.scalar.copy
+                copy(
                     out=grouped_words[:, two * 2 * P : (two + 1) * 2 * P, :].rearrange(
                         "p (b r) u -> p b r u", b=2
                     ),
@@ -260,33 +262,37 @@ def tile_tropicalattention_pa_t_kernel(
             )
             return z
 
-        def relu_plus_one(out, z):
-            nc.vector.tensor_scalar(
-                out=out, in0=z, scalar1=0.0, scalar2=1.0, op0=ALU.max, op1=ALU.add
-            )
+        def relu(out, z, first=False):
+            if first:
+                nc.vector.tensor_scalar(
+                    out=out, in0=z, scalar1=0.0, scalar2=None, op0=ALU.max
+                )
+            else:
+                nc.scalar.activation(out=out, in_=z, func=ACT.Relu)
 
-        def log_steps(j, parts):
+        def log_one_plus(out, in_):
+            nc.scalar.activation(out=out, in_=in_, func=ACT.Ln, bias=1.0)
+
+        def log_steps(j, parts, first=False):
             g_lo = logs.tile([P, len(parts) * PART], F32)
             g_step = logs.tile([P, len(parts) * PART], F32)
 
-            def log_half(n, a):
+            def log_part(n):
                 cols = slice(n * PART, (n + 1) * PART)
-                grown = tokens.tile([P, PART], F32)
-                z = mx_pass(parts[n], w_codes[:, j, a, :], w_scales[:, j, a, :])
-                relu_plus_one(grown[:], z[:])
-                if a == 0:
-                    nc.scalar.activation(out=g_lo[:, cols], in_=grown[:], func=ACT.Ln)
-                else:
-                    g_hi = tokens.tile([P, PART], F32)
-                    nc.scalar.activation(out=g_hi[:], in_=grown[:], func=ACT.Ln)
-                    nc.gpsimd.tensor_tensor(
-                        out=g_step[:, cols], in0=g_hi[:], in1=g_lo[:, cols], op=ALU.subtract
-                    )
+                z_lo = mx_pass(parts[n], w_codes[:, j, 0, :], w_scales[:, j, 0, :])
+                z_hi = mx_pass(parts[n], w_codes[:, j, 1, :], w_scales[:, j, 1, :])
+                grown_lo = tokens.tile([P, PART], F32)
+                grown_hi = tokens.tile([P, PART], F32)
+                g_hi = tokens.tile([P, PART], F32)
+                relu(grown_lo[:], z_lo[:], first)
+                relu(grown_hi[:], z_hi[:], first)
+                log_one_plus(g_lo[:, cols], grown_lo[:])
+                log_one_plus(g_hi[:], grown_hi[:])
+                nc.gpsimd.tensor_tensor(
+                    out=g_step[:, cols], in0=g_hi[:], in1=g_lo[:, cols], op=ALU.subtract
+                )
 
-            steps = [
-                lambda n=n, a=a: log_half(n, a) for n in range(len(parts)) for a in range(2)
-            ]
-            return g_lo, g_step, steps
+            return g_lo, g_step, [lambda n=n: log_part(n) for n in range(len(parts))]
 
         banks_done = [0]
         events = {}
@@ -355,23 +361,19 @@ def tile_tropicalattention_pa_t_kernel(
             base = quad.tile([P, PART], F32)
             spread = quad.tile([P, PART], F32)
             kept_rows = {}
-            grown_of = {}
 
-            def log_quarter(f, g):
+            def log_quarter(f):
                 parts = QUAD_PARTS[s]
-                rows = slice(0, P) if len(parts) == 1 else slice(g * DK, (g + 1) * DK)
-                if g == 0:
-                    grown = tokens.tile([P, PART], F32)
-                    grown_of[f] = grown
-                z = mx_pass(parts[g], quad_codes[:, s, f, :], quad_scales[:, s, f, :])
-                relu_plus_one(grown_of[f][rows, :], z[rows, :])
-                if g < len(parts) - 1:
-                    return
+                grown = quad.tile([P, PART], F32)
+                for g, part in enumerate(parts):
+                    rows = slice(0, P) if len(parts) == 1 else slice(g * DK, (g + 1) * DK)
+                    z = mx_pass(part, quad_codes[:, s, f, :], quad_scales[:, s, f, :])
+                    relu(grown[rows, :], z[rows, :])
                 if f == 0:
-                    nc.scalar.activation(out=base[:], in_=grown_of[f][:], func=ACT.Ln)
+                    log_one_plus(base[:], grown[:])
                     return
                 g_hi = tokens.tile([P, PART], F32)
-                nc.scalar.activation(out=g_hi[:], in_=grown_of[f][:], func=ACT.Ln)
+                log_one_plus(g_hi[:], grown[:])
                 if f == 1:
                     step = spread
                 else:
@@ -386,7 +388,7 @@ def tile_tropicalattention_pa_t_kernel(
                         turned[:, b, :], kept_rows[f][:, b * P : (b + 1) * P], ident[:]
                     )
                 by_token = quad.tile([P, PART_BLOCKS, P], F32)
-                nc.vector.tensor_copy(out=by_token[:], in_=turned[:])
+                nc.scalar.copy(out=by_token[:], in_=turned[:])
                 kept_rows[f] = by_token
 
             def keep():
@@ -400,8 +402,7 @@ def tile_tropicalattention_pa_t_kernel(
 
             stage["base"] = base
             stage["spread"] = spread
-            passes = [(f, g) for f in range(4) for g in range(len(QUAD_PARTS[s]))]
-            logs_first = [lambda f=f, g=g: log_quarter(f, g) for f, g in passes]
+            logs_first = [lambda f=f: log_quarter(f) for f in range(4)]
             turns = [lambda f=f: turn_step(f) for f in (2, 3)]
             return logs_first, turns, keep, stage
 
@@ -415,10 +416,16 @@ def tile_tropicalattention_pa_t_kernel(
                     bias=quad_cols[:, s, 1, o : o + 1], scale=1.0,
                 )
                 first = quad_units.tile([P, PART], F32)
-                nc.scalar.activation(
-                    out=first[:], in_=stage["base"][:], func=ACT.Identity,
-                    bias=quad_cols[:, s, 0, o : o + 1], scale=1.0,
-                )
+                if o % GPSIMD_BASES_OF < GPSIMD_BASES:
+                    nc.gpsimd.tensor_scalar(
+                        out=first[:], in0=stage["base"][:], scalar1=quad_cols[:, s, 0, o : o + 1],
+                        scalar2=1.0, op0=ALU.add, op1=ALU.mult,
+                    )
+                else:
+                    nc.scalar.activation(
+                        out=first[:], in_=stage["base"][:], func=ACT.Identity,
+                        bias=quad_cols[:, s, 0, o : o + 1], scale=1.0,
+                    )
                 tiles["lead"], tiles["first"] = lead, first
 
             def grow(f):
@@ -505,13 +512,13 @@ def tile_tropicalattention_pa_t_kernel(
             for step in x_steps(part):
                 step()
         j, parts = STAGES[0]
-        g_lo, g_step, log_parts = log_steps(j, parts)
-        for step in log_parts[: 2 * head_parts]:
+        g_lo, g_step, log_parts = log_steps(j, parts, first=True)
+        for step in log_parts[:head_parts]:
             step()
         with tc.manual_schedule(engines={mybir.EngineType.DVE}):
             for part in parts[head_parts:]:
                 todo.extend(x_steps(part))
-            todo.extend(log_parts[2 * head_parts :])
+            todo.extend(log_parts[head_parts:])
             for stage, (j, parts) in enumerate(STAGES):
                 blocks = range(len(parts) * PART_BLOCKS)
                 halves = [range(0, len(blocks) // 2), range(len(blocks) // 2, len(blocks))]

@@ -277,22 +277,23 @@ def tile_tropicalattention_pa_t_kernel(
             g_lo = logs.tile([P, len(parts) * PART], F32)
             g_step = logs.tile([P, len(parts) * PART], F32)
 
-            def log_part(n):
+            def log_half(n, a):
                 cols = slice(n * PART, (n + 1) * PART)
-                z_lo = mx_pass(parts[n], w_codes[:, j, 0, :], w_scales[:, j, 0, :])
-                z_hi = mx_pass(parts[n], w_codes[:, j, 1, :], w_scales[:, j, 1, :])
-                grown_lo = tokens.tile([P, PART], F32)
-                grown_hi = tokens.tile([P, PART], F32)
-                g_hi = tokens.tile([P, PART], F32)
-                relu(grown_lo[:], z_lo[:], first)
-                relu(grown_hi[:], z_hi[:], first)
-                log_one_plus(g_lo[:, cols], grown_lo[:])
-                log_one_plus(g_hi[:], grown_hi[:])
-                nc.gpsimd.tensor_tensor(
-                    out=g_step[:, cols], in0=g_hi[:], in1=g_lo[:, cols], op=ALU.subtract
-                )
+                z = mx_pass(parts[n], w_codes[:, j, a, :], w_scales[:, j, a, :])
+                grown = tokens.tile([P, PART], F32)
+                relu(grown[:], z[:], first)
+                if a == 0:
+                    log_one_plus(g_lo[:, cols], grown[:])
+                else:
+                    g_hi = tokens.tile([P, PART], F32)
+                    log_one_plus(g_hi[:], grown[:])
+                    nc.gpsimd.tensor_tensor(
+                        out=g_step[:, cols], in0=g_hi[:], in1=g_lo[:, cols], op=ALU.subtract
+                    )
 
-            return g_lo, g_step, [lambda n=n: log_part(n) for n in range(len(parts))]
+            return g_lo, g_step, [
+                lambda n=n, a=a: log_half(n, a) for n in range(len(parts)) for a in range(2)
+            ]
 
         banks_done = [0]
         events = {}
@@ -362,13 +363,19 @@ def tile_tropicalattention_pa_t_kernel(
             spread = quad.tile([P, PART], F32)
             kept_rows = {}
 
-            def log_quarter(f):
+            grown_of = {}
+
+            def log_quarter(f, g):
                 parts = QUAD_PARTS[s]
-                grown = quad.tile([P, PART], F32)
-                for g, part in enumerate(parts):
-                    rows = slice(0, P) if len(parts) == 1 else slice(g * DK, (g + 1) * DK)
-                    z = mx_pass(part, quad_codes[:, s, f, :], quad_scales[:, s, f, :])
-                    relu(grown[rows, :], z[rows, :])
+                if g == 0:
+                    grown = quad.tile([P, PART], F32)
+                    grown_of[f] = grown
+                grown = grown_of[f]
+                rows = slice(0, P) if len(parts) == 1 else slice(g * DK, (g + 1) * DK)
+                z = mx_pass(parts[g], quad_codes[:, s, f, :], quad_scales[:, s, f, :])
+                relu(grown[rows, :], z[rows, :])
+                if g < len(parts) - 1:
+                    return
                 if f == 0:
                     log_one_plus(base[:], grown[:])
                     return
@@ -402,7 +409,11 @@ def tile_tropicalattention_pa_t_kernel(
 
             stage["base"] = base
             stage["spread"] = spread
-            logs_first = [lambda f=f: log_quarter(f) for f in range(4)]
+            logs_first = [
+                lambda f=f, g=g: log_quarter(f, g)
+                for f in range(4)
+                for g in range(len(QUAD_PARTS[s]))
+            ]
             turns = [lambda f=f: turn_step(f) for f in (2, 3)]
             return logs_first, turns, keep, stage
 
@@ -477,6 +488,20 @@ def tile_tropicalattention_pa_t_kernel(
                 events.setdefault(bank, []).append(piece)
             return first_bank + (DK - 1) * QUAD_EVERY + 6
 
+        def merge(regular, others):
+            steps = []
+            regular, others = list(regular), list(others)
+            while regular or others:
+                if regular and len(steps) % 6 == 3:
+                    steps.append(regular[0])
+                    regular = regular[1:]
+                elif others:
+                    steps.append(others[0])
+                    others = others[1:]
+                else:
+                    steps.append(lambda: None)
+            return steps
+
         todo = []
         taken = [0]
 
@@ -505,43 +530,43 @@ def tile_tropicalattention_pa_t_kernel(
 
         def prepare_quads(s, between):
             logs_first, turns, keep, stage = quad_steps(s)
-            todo.extend(logs_first + between + turns)
-            todo.append(lambda: start_quads(s, stage, keep))
+            return logs_first + between + turns + [lambda: start_quads(s, stage, keep)]
 
         for part in range(1, head_parts):
             for step in x_steps(part):
                 step()
         j, parts = STAGES[0]
         g_lo, g_step, log_parts = log_steps(j, parts, first=True)
-        for step in log_parts[:head_parts]:
+        for step in log_parts[: 2 * head_parts]:
             step()
         with tc.manual_schedule(engines={mybir.EngineType.DVE}):
             for part in parts[head_parts:]:
                 todo.extend(x_steps(part))
-            todo.extend(log_parts[head_parts:])
+            todo.extend(log_parts[2 * head_parts :])
             for stage, (j, parts) in enumerate(STAGES):
                 blocks = range(len(parts) * PART_BLOCKS)
                 halves = [range(0, len(blocks) // 2), range(len(blocks) // 2, len(blocks))]
                 y = results.tile([P, len(blocks), HEADS, DK], F32)
                 start_o = 0
+                others = []
                 if stage == 0:
                     sweep(g_lo, g_step, j, range(edge), y, halves[0])
                     finish_steps()
                     start_o = edge
                     for f in range(4):
                         quad_weights(0, f)
-                    todo.extend(x_steps(7))
+                    others.extend(x_steps(7))
                     constants = [lambda g=g: quad_constants(g) for g in range(2)]
                     constants += [lambda s=s: quad_turn_constants(s) for s in range(2)]
-                    prepare_quads(0, constants + pause(2))
-                if stage + 1 < len(STAGES):
-                    next_lo, next_step, log_parts = log_steps(*STAGES[stage + 1])
-                    todo.extend(log_parts)
+                    others.extend(prepare_quads(0, constants + pause(2)))
                 if stage == 1:
                     for part in (4, 5, 6):
-                        todo.extend(x_steps(part))
-                    todo.extend([lambda f=f: quad_weights(1, f) for f in range(4)])
-                    prepare_quads(1, pause(6))
+                        others.extend(x_steps(part))
+                    others.extend([lambda f=f: quad_weights(1, f) for f in range(4)])
+                    others.extend(prepare_quads(1, pause(6)))
+                if stage + 1 < len(STAGES):
+                    next_lo, next_step, log_parts = log_steps(*STAGES[stage + 1])
+                    todo.extend(merge(log_parts, others))
                 if stage == 0:
                     sweep(g_lo, g_step, j, range(edge), y, halves[1])
                 if stage + 1 < len(STAGES):

@@ -124,8 +124,9 @@ def tile_tropicalattention_pa_t_kernel(
                 quantise
             ]
 
-        for step in x_steps(0):
-            step()
+        for part in range(2):
+            for step in x_steps(part):
+                step()
 
         w_codes = const.tile([P, PROJ, 2, P], U32, align_bytes=64)
         w_scales = const.tile([P, PROJ, 2, P], U8, align_bytes=64)
@@ -502,6 +503,9 @@ def tile_tropicalattention_pa_t_kernel(
                     steps.append(lambda: None)
             return steps
 
+        def warm_up():
+            mx_pass(0, w_codes[:, 0, 0, :], w_scales[:, 0, 0, :])
+
         todo = []
         taken = [0]
 
@@ -532,9 +536,6 @@ def tile_tropicalattention_pa_t_kernel(
             logs_first, turns, keep, stage = quad_steps(s)
             return logs_first + between + turns + [lambda: start_quads(s, stage, keep)]
 
-        for part in range(1, head_parts):
-            for step in x_steps(part):
-                step()
         j, parts = STAGES[0]
         g_lo, g_step, log_parts = log_steps(j, parts, first=True)
         for step in log_parts[: 2 * head_parts]:
@@ -566,7 +567,9 @@ def tile_tropicalattention_pa_t_kernel(
                     others.extend(prepare_quads(1, pause(6)))
                 if stage + 1 < len(STAGES):
                     next_lo, next_step, log_parts = log_steps(*STAGES[stage + 1])
-                    todo.extend(merge(log_parts, others))
+                    todo.extend(merge(log_parts + [warm_up] * 2, others))
+                else:
+                    todo.extend(merge([warm_up] * 10, others))
                 if stage == 0:
                     sweep(g_lo, g_step, j, range(edge), y, halves[1])
                 if stage + 1 < len(STAGES):

@@ -489,19 +489,17 @@ def tile_tropicalattention_pa_t_kernel(
                 events.setdefault(bank, []).append(piece)
             return first_bank + (DK - 1) * QUAD_EVERY + 6
 
-        def merge(regular, others):
-            steps = []
-            regular, others = list(regular), list(others)
-            while regular or others:
-                if regular and len(steps) % 6 == 3:
-                    steps.append(regular[0])
-                    regular = regular[1:]
-                elif others:
-                    steps.append(others[0])
-                    others = others[1:]
-                else:
-                    steps.append(lambda: None)
-            return steps
+        def together(*steps):
+            def run():
+                for step in steps:
+                    step()
+            return run
+
+        def spread(steps, every):
+            spaced = []
+            for step in steps:
+                spaced += [step] + pause(every - 1)
+            return spaced
 
         def warm_up():
             mx_pass(0, w_codes[:, 0, 0, :], w_scales[:, 0, 0, :])
@@ -534,42 +532,62 @@ def tile_tropicalattention_pa_t_kernel(
 
         def prepare_quads(s, between):
             logs_first, turns, keep, stage = quad_steps(s)
-            return logs_first + between + turns + [lambda: start_quads(s, stage, keep)]
+            return logs_first, between + turns + [lambda: start_quads(s, stage, keep)]
 
         j, parts = STAGES[0]
         g_lo, g_step, log_parts = log_steps(j, parts, first=True)
         for step in log_parts[: 2 * head_parts]:
             step()
-        with tc.manual_schedule(engines={mybir.EngineType.DVE}):
-            for part in parts[head_parts:]:
-                todo.extend(x_steps(part))
-            todo.extend(log_parts[2 * head_parts :])
+        with tc.manual_schedule(engines={mybir.EngineType.DVE, mybir.EngineType.PE}):
+            a0, a1, a2 = x_steps(2)
+            b0, b1, b2 = x_steps(3)
+            todo.extend([together(a0, warm_up), together(a1, warm_up), together(b0, warm_up)])
+            todo.extend([together(b1, warm_up, a2), pause(1)[0]])
+            todo.extend(log_parts[4:6] + [b2] + pause(1) + log_parts[6:])
             for stage, (j, parts) in enumerate(STAGES):
                 blocks = range(len(parts) * PART_BLOCKS)
                 halves = [range(0, len(blocks) // 2), range(len(blocks) // 2, len(blocks))]
                 y = results.tile([P, len(blocks), HEADS, DK], F32)
                 start_o = 0
-                others = []
                 if stage == 0:
                     sweep(g_lo, g_step, j, range(edge), y, halves[0])
                     finish_steps()
                     start_o = edge
                     for f in range(4):
                         quad_weights(0, f)
-                    others.extend(x_steps(7))
-                    constants = [lambda g=g: quad_constants(g) for g in range(2)]
-                    constants += [lambda s=s: quad_turn_constants(s) for s in range(2)]
-                    others.extend(prepare_quads(0, constants + pause(2)))
-                if stage == 1:
-                    for part in (4, 5, 6):
-                        others.extend(x_steps(part))
-                    others.extend([lambda f=f: quad_weights(1, f) for f in range(4)])
-                    others.extend(prepare_quads(1, pause(6)))
                 if stage + 1 < len(STAGES):
                     next_lo, next_step, log_parts = log_steps(*STAGES[stage + 1])
-                    todo.extend(merge(log_parts + [warm_up] * 2, others))
+                if stage == 0:
+                    constants = [lambda g=g: quad_constants(g) for g in range(2)]
+                    constants += [lambda s=s: quad_turn_constants(s) for s in range(2)]
+                    quad_logs, quad_rest = prepare_quads(0, constants + pause(2))
+                    a0, a1, a2 = x_steps(7)
+                    todo.extend([together(a0, log_parts[0]), together(a1, log_parts[1])])
+                    todo.extend(pause(1) + [together(log_parts[2], a2)] + pause(1))
+                    todo.extend(quad_logs + quad_rest + spread(log_parts[3:], 6))
+                elif stage == 1:
+                    quad_logs, quad_rest = prepare_quads(1, pause(4))
+                    a0, a1, a2 = x_steps(6)
+                    b0, b1, b2 = x_steps(4)
+                    c0, c1, c2 = x_steps(5)
+                    todo.extend(spread([
+                        together(a0, log_parts[0]),
+                        together(a1, log_parts[1]),
+                        together(b0, log_parts[2], a2),
+                        together(b1, log_parts[3]),
+                        together(c0, log_parts[4], b2),
+                        together(c1, log_parts[5]),
+                        together(log_parts[6], c2),
+                        log_parts[7],
+                    ], 5))
+                    todo.extend([lambda f=f: quad_weights(1, f) for f in range(4)])
+                    todo.extend(spread(quad_logs, 2))
+                elif stage == 2:
+                    todo.extend(quad_rest + spread(log_parts, 7))
+                elif stage + 1 < len(STAGES):
+                    todo.extend(spread(log_parts, 8))
                 else:
-                    todo.extend(merge([warm_up] * 10, others))
+                    todo.extend(pause(4) + spread([warm_up] * 6, 8))
                 if stage == 0:
                     sweep(g_lo, g_step, j, range(edge), y, halves[1])
                 if stage + 1 < len(STAGES):

import concourse.mybir as mybir
from concourse.masks import make_identity

F32 = mybir.dt.float32
BF16 = mybir.dt.bfloat16
I32 = mybir.dt.int32
U32 = mybir.dt.uint32
U8 = mybir.dt.uint8
FP8X4 = mybir.dt.float8_e4m3fn_x4
ACT = mybir.ActivationFunctionType
ALU = mybir.AluOpType
X_AXIS = mybir.AxisListType.X


P = 128
TOKENS = 16 * 256
BATCH_LEN = 256
D = 512
HEADS = 4
DK = 64
HALF = DK // 2
QUARTER = DK // 4
E = HEADS * DK
PROJ = 3
BANK = 512
BANK_BLOCKS = BANK // P
PART = 512
PARTS = TOKENS // PART
PART_BLOCKS = PART // P
RELU_BLOCKS = 8
LOG_LIMIT = 89.0

STAGES = [
    (0, [0, 1, 2, 3]),
    (1, [0, 1, 2, 3]),
    (2, [0, 1, 2, 3]),
    (0, [4, 5, 6]),
    (1, [4, 5, 6]),
    (2, [4, 5]),
]
QUAD_PARTS = [[7], [6, 7]]
QUAD_EVERY = 9
GPSIMD_BASES, GPSIMD_BASES_OF = 3, 8

FLOPS = 2 * TOKENS * D * PROJ * E + 2 * TOKENS * PROJ * E * DK


def tile_tropicalattention_pa_t_kernel(
    tc,
    x,
    Wq_words,
    Wq_scales,
    Wk_words,
    Wk_scales,
    Wv_words,
    Wv_scales,
    lam,
    Wq_trop,
    Wk_trop,
    Wv_trop,
    out_0,
    out_1,
    out_2,
):
    nc = tc.nc
    x_rows = x.flatten_outer_dims()
    outs = [out_0, out_1, out_2]

    with (
        tc.tile_pool(name="const", bufs=1) as const,
        tc.tile_pool(name="tokens", bufs=2) as tokens,
        tc.tile_pool(name="coded", bufs=PARTS) as coded,
        tc.tile_pool(name="logs", bufs=2) as logs,
        tc.tile_pool(name="lows", bufs=4) as lows,
        tc.tile_pool(name="relus", bufs=6) as relus,
        tc.tile_pool(name="results", bufs=2) as results,
        tc.tile_pool(name="quad", bufs=2) as quad,
        tc.tile_pool(name="quad_units", bufs=4) as quad_units,
        tc.tile_pool(name="quad_results", bufs=1) as quad_results,
        tc.psum_pool(name="banks", bufs=6) as banks,
        tc.psum_pool(name="kept_banks", bufs=1) as kept_banks,
    ):
        ident = const.tile([P, P], F32)
        make_identity(nc, ident[:])

        codes = {}

        def x_steps(part):
            x_sb = tokens.tile([P, PART_BLOCKS, D], BF16)
            nc.sync.dma_start(
                out=x_sb[:],
                in_=x_rows[part * PART : (part + 1) * PART, :].rearrange("(b p) k -> p b k", p=P),
            )
            grouped = tokens.tile([P, PART, 4], BF16, align_bytes=64)
            grouped_words = grouped[:].bitcast(F32)
            x_codes = coded.tile([P, PART], U32, align_bytes=64)
            x_scales = coded.tile([P, PART], U8, align_bytes=64)
            codes[part] = (x_codes, x_scales)

            def turn_two_blocks(two):
                turned = banks.tile([P, 2, 2, P], F32, tag="bank")
                for b in range(2):
                    x_words = x_sb[:, 2 * two + b, :].bitcast(F32)
                    for u in range(2):
                        nc.tensor.transpose(
                            turned[:, b, u, :], x_words[:, u : D // 2 : 2], ident[:]
                        )
                copy = nc.vector.tensor_copy if part in STAGES[0][1] else nc.scalar.copy
                copy(
                    out=grouped_words[:, two * 2 * P : (two + 1) * 2 * P, :].rearrange(
                        "p (b r) u -> p b r u", b=2
                    ),
                    in_=turned[:].rearrange("p b u r -> p b r u"),
                )

            def quantise():
                nc.vector.quantize_mx(
                    out=x_codes[:].bitcast(FP8X4),
                    scales=x_scales[:],
                    in_=grouped[:].rearrange("p r t -> p (r t)"),
                )

            return [lambda two=two: turn_two_blocks(two) for two in range(PART_BLOCKS // 2)] + [
                quantise
            ]

        for part in range(2):
            for step in x_steps(part):
                step()

        w_codes = const.tile([P, PROJ, 2, P], U32, align_bytes=64)
        w_scales = const.tile([P, PROJ, 2, P], U8, align_bytes=64)
        nc.vector.memset(w_scales[:].bitcast(I32), 0)
        weights = [(Wq_words, Wq_scales), (Wk_words, Wk_scales), (Wv_words, Wv_scales)]
        for j, (words, scales) in enumerate(weights):
            words_by_half = (
                words[0]
                .rearrange("p n t -> p (n t)")
                .bitcast(I32)
                .rearrange("p (h a i) -> p a h i", a=2, i=HALF)
            )
            for a in range(2):
                nc.sync.dma_start(
                    out=w_codes[:, j, a, :].bitcast(I32).rearrange("p (h i) -> p h i", h=HEADS),
                    in_=words_by_half[:, a, :, :],
                )
            for quadrant in range(4):
                rows_by_half = (
                    scales[0, 4 * quadrant : 4 * quadrant + 4, :]
                    .bitcast(I32)
                    .rearrange("r (h a w) -> r a h w", a=2, w=HALF // 4)
                )
                for a in range(2):
                    nc.sync.dma_start(
                        out=w_scales[32 * quadrant : 32 * quadrant + 4, j, a, :]
                        .bitcast(I32)
                        .rearrange("r (h w) -> r h w", h=HEADS),
                        in_=rows_by_half[:, a, :, :],
                    )

        t_rows = const.tile([P, 2, DK], BF16)
        nc.scalar.dma_start(out=t_rows[0:DK, 0, :], in_=Wq_trop)
        nc.scalar.dma_start(out=t_rows[DK:P, 0, :], in_=Wk_trop)
        nc.scalar.dma_start(out=t_rows[0:DK, 1, :], in_=Wv_trop)
        nc.scalar.dma_start(out=t_rows[DK:P, 1, :], in_=Wv_trop)
        lam_rows = const.tile([P, E], BF16)
        nc.scalar.dma_start(
            out=lam_rows[:], in_=lam.rearrange("a b n -> (a b n)").partition_broadcast(P)
        )
        c = const.tile([P, 2, HEADS, DK], F32)
        for square in range(2):
            nc.vector.tensor_tensor(
                out=c[:, square, :, :],
                in0=t_rows[:, square, :].unsqueeze(1).to_broadcast([P, HEADS, DK]),
                in1=lam_rows[:].rearrange("p (h i) -> p h i", h=HEADS),
                op=ALU.subtract,
            )
        c_floor = const.tile([P, 2, HEADS], F32)
        nc.vector.tensor_reduce(out=c_floor[:], in_=c[:], axis=X_AXIS, op=ALU.max)
        nc.vector.tensor_scalar(
            out=c_floor[:], in0=c_floor[:], scalar1=-LOG_LIMIT, scalar2=None, op0=ALU.add
        )
        nc.vector.tensor_tensor(
            out=c[:],
            in0=c[:],
            in1=c_floor[:].unsqueeze(3).to_broadcast([P, 2, HEADS, DK]),
            op=ALU.max,
        )
        c_rows = const.tile([P, 2, 2, HEADS, HALF], F32)
        nc.vector.tensor_copy(out=c_rows[:, 0, :, :, :], in_=c[:, :, :, 0:HALF])
        nc.vector.tensor_sub(
            out=c_rows[:, 1, :, :, :], in0=c[:, :, :, HALF:DK], in1=c[:, :, :, 0:HALF]
        )
        c_turned = banks.tile([P, 2, 2, P], F32, tag="bank")
        for kind in range(2):
            for square in range(2):
                nc.tensor.transpose(
                    c_turned[:, kind, square, :],
                    c_rows[:, kind, square, :, :].rearrange("p h i -> p (h i)"),
                    ident[:],
                )
        c_cols = const.tile([P, 2, 2 * P], F32)
        nc.vector.tensor_copy(out=c_cols[:], in_=c_turned[:].rearrange("p k s o -> p k (s o)"))

        quad_codes = const.tile([P, 2, 4, P], U32, align_bytes=64)
        quad_scales = const.tile([P, 2, 4, P], U8, align_bytes=64)
        quad_rows = const.tile([P, 2, 4, 2, HEADS, QUARTER], F32)
        quad_cols = const.tile([P, 2, 4, DK], F32)

        def quad_weights(s, f):
            a, i0 = f // 2, (f % 2) * QUARTER
            codes_from = w_codes[:].bitcast(I32).rearrange("p j a (h i) -> p j a h i", h=HEADS)
            scales_from = w_scales[:].bitcast(I32).rearrange("p j a (h w) -> p j a h w", h=HEADS)
            codes_to = quad_codes[:, s, f, :].bitcast(I32).rearrange(
                "p (g h i) -> p g h i", g=2, h=HEADS
            )
            scales_to = quad_scales[:, s, f, :].bitcast(I32).rearrange(
                "p (g h w) -> p g h w", g=2, h=HEADS
            )
            for g in range(2):
                j = 2 if s == 1 else g
                nc.gpsimd.tensor_copy(
                    out=codes_to[:, g, :, :], in_=codes_from[:, j, a, :, i0 : i0 + QUARTER]
                )
                nc.gpsimd.tensor_copy(
                    out=scales_to[:, g, :, :],
                    in_=scales_from[:, j, a, :, i0 // 4 : (i0 + QUARTER) // 4],
                )

        def quad_constants(g):
            for s in range(2):
                nc.vector.tensor_copy(out=quad_rows[:, s, 0, g, :, :], in_=c[:, s, :, 0:QUARTER])
            for f in range(1, 4):
                nc.vector.tensor_sub(
                    out=quad_rows[:, :, f, g, :, :],
                    in0=c[:, :, :, f * QUARTER : (f + 1) * QUARTER],
                    in1=c[:, :, :, 0:QUARTER],
                )

        def quad_turn_constants(s):
            turned = banks.tile([P, 4, P], F32, tag="bank")
            for kind in range(4):
                nc.tensor.transpose(
                    turned[:, kind, :],
                    quad_rows[:, s, kind, :, :, :].rearrange("p g h i -> p (g h i)"),
                    ident[:],
                )
            for g in range(2):
                rows = slice(g * DK, (g + 1) * DK)
                nc.vector.tensor_copy(out=quad_cols[rows, s, :, :], in_=turned[rows, :, rows])

        def mx_pass(part, lhs_codes, lhs_scales):
            x_codes, x_scales = codes[part]
            z = banks.tile([P, BANK], F32, tag="bank")
            nc.tensor.matmul_mx(
                out=z[:],
                lhsT=lhs_codes.bitcast(FP8X4),
                lhsT_scale=lhs_scales,
                rhs=x_codes[:].bitcast(FP8X4),
                rhs_scale=x_scales[:],
                start=True,
                stop=True,
            )
            return z

        def relu(out, z, first=False):
            if first:
                nc.vector.tensor_scalar(
                    out=out, in0=z, scalar1=0.0, scalar2=None, op0=ALU.max
                )
            else:
                nc.scalar.activation(out=out, in_=z, func=ACT.Relu)

        def log_one_plus(out, in_):
            nc.scalar.activation(out=out, in_=in_, func=ACT.Ln, bias=1.0)

        def log_steps(j, parts, first=False):
            g_lo = logs.tile([P, len(parts) * PART], F32)
            g_step = logs.tile([P, len(parts) * PART], F32)

            def log_half(n, a):
                cols = slice(n * PART, (n + 1) * PART)
                z = mx_pass(parts[n], w_codes[:, j, a, :], w_scales[:, j, a, :])
                grown = tokens.tile([P, PART], F32)
                relu(grown[:], z[:], first)
                if a == 0:
                    log_one_plus(g_lo[:, cols], grown[:])
                else:
                    g_hi = tokens.tile([P, PART], F32)
                    log_one_plus(g_hi[:], grown[:])
                    nc.gpsimd.tensor_tensor(
                        out=g_step[:, cols], in0=g_hi[:], in1=g_lo[:, cols], op=ALU.subtract
                    )

            return g_lo, g_step, [
                lambda n=n, a=a: log_half(n, a) for n in range(len(parts)) for a in range(2)
            ]

        banks_done = [0]
        events = {}

        def tick():
            banks_done[0] += 1
            for work in events.get(banks_done[0], []):
                work()

        def tropical(g_lo, g_step, j, o, y, blocks):
            col = j * DK + o
            sum_lo = lows.tile([P, len(blocks) * P], F32)
            nc.gpsimd.tensor_scalar(
                out=sum_lo[:], in0=g_lo[:, blocks.start * P : blocks.stop * P],
                scalar1=c_cols[:, 0, col : col + 1],
                scalar2=1.0, op0=ALU.add, op1=ALU.mult,
            )
            for r0 in range(0, len(blocks), RELU_BLOCKS):
                width = min(RELU_BLOCKS, len(blocks) - r0)
                first = blocks.start + r0
                excess = relus.tile([P, width * P], F32)
                nc.scalar.activation(
                    out=excess[:], in_=g_step[:, first * P : (first + width) * P], func=ACT.Relu,
                    bias=c_cols[:, 1, col : col + 1], scale=1.0,
                )
                for b0 in range(0, width, BANK_BLOCKS):
                    pair_max = banks.tile([P, BANK_BLOCKS, P], F32, tag="bank")
                    for b in range(BANK_BLOCKS):
                        nc.tensor.matmul(
                            out=pair_max[:, b, :],
                            lhsT=sum_lo[:, (r0 + b0 + b) * P : (r0 + b0 + b + 1) * P],
                            rhs=ident[:], start=True, stop=False, is_transpose=True,
                        )
                        nc.tensor.matmul(
                            out=pair_max[:, b, :],
                            lhsT=excess[:, (b0 + b) * P : (b0 + b + 1) * P],
                            rhs=ident[:], start=False, stop=True, is_transpose=True,
                        )
                    nc.vector.tensor_reduce(
                        out=y[:, first + b0 : first + b0 + BANK_BLOCKS, :, o],
                        in_=pair_max[:].rearrange("p b (h i) -> p b h i", h=HEADS),
                        axis=X_AXIS,
                        op=ALU.max,
                    )
                    tick()

        def store(j, parts, y, blocks):
            for b in blocks:
                first = parts[b // PART_BLOCKS] * PART + (b % PART_BLOCKS) * P
                store_block(j, first, y[:, b, :, :])

        def store_block(j, first, rows):
            batch, l0 = first // BATCH_LEN, first % BATCH_LEN
            nc.sync.dma_start(
                out=outs[j][batch * HEADS : (batch + 1) * HEADS, l0 : l0 + P, :].rearrange(
                    "h l o -> l h o"
                ),
                in_=rows,
            )

        def pause(steps):
            return [lambda: None for step in range(steps)]

        def quad_steps(s):
            stage = {}
            base = quad.tile([P, PART], F32)
            spread = quad.tile([P, PART], F32)
            kept_rows = {}

            grown_of = {}

            def log_quarter(f, g):
                parts = QUAD_PARTS[s]
                if g == 0:
                    grown = quad.tile([P, PART], F32)
                    grown_of[f] = grown
                grown = grown_of[f]
                rows = slice(0, P) if len(parts) == 1 else slice(g * DK, (g + 1) * DK)
                z = mx_pass(parts[g], quad_codes[:, s, f, :], quad_scales[:, s, f, :])
                relu(grown[rows, :], z[rows, :])
                if g < len(parts) - 1:
                    return
                if f == 0:
                    log_one_plus(base[:], grown[:])
                    return
                g_hi = tokens.tile([P, PART], F32)
                log_one_plus(g_hi[:], grown[:])
                if f == 1:
                    step = spread
                else:
                    step = quad.tile([P, PART], F32)
                    kept_rows[f] = step
                nc.gpsimd.tensor_tensor(out=step[:], in0=g_hi[:], in1=base[:], op=ALU.subtract)

            def turn_step(f):
                turned = banks.tile([P, PART_BLOCKS, P], F32, tag="bank")
                for b in range(PART_BLOCKS):
                    nc.tensor.transpose(
                        turned[:, b, :], kept_rows[f][:, b * P : (b + 1) * P], ident[:]
                    )
                by_token = quad.tile([P, PART_BLOCKS, P], F32)
                nc.scalar.copy(out=by_token[:], in_=turned[:])
                kept_rows[f] = by_token

            def keep():
                for f in (2, 3):
                    kept = kept_banks.tile([P, PART], F32, tag="kept%d" % f)
                    for b in range(PART_BLOCKS):
                        nc.tensor.transpose(
                            kept[:, b * P : (b + 1) * P], kept_rows[f][:, b, :], ident[:]
                        )
                    stage[f] = kept

            stage["base"] = base
            stage["spread"] = spread
            logs_first = [
                lambda f=f, g=g: log_quarter(f, g)
                for f in range(4)
                for g in range(len(QUAD_PARTS[s]))
            ]
            turns = [lambda f=f: turn_step(f) for f in (2, 3)]
            return logs_first, turns, keep, stage

        def quad_unit(s, stage, o):
            tiles = {}

            def feed():
                lead = quad_units.tile([P, PART], F32)
                nc.scalar.activation(
                    out=lead[:], in_=stage["spread"][:], func=ACT.Relu,
                    bias=quad_cols[:, s, 1, o : o + 1], scale=1.0,
                )
                first = quad_units.tile([P, PART], F32)
                if o % GPSIMD_BASES_OF < GPSIMD_BASES:
                    nc.gpsimd.tensor_scalar(
                        out=first[:], in0=stage["base"][:], scalar1=quad_cols[:, s, 0, o : o + 1],
                        scalar2=1.0, op0=ALU.add, op1=ALU.mult,
                    )
                else:
                    nc.scalar.activation(
                        out=first[:], in_=stage["base"][:], func=ACT.Identity,
                        bias=quad_cols[:, s, 0, o : o + 1], scale=1.0,
                    )
                tiles["lead"], tiles["first"] = lead, first

            def grow(f):
                lead = tiles["lead"]
                nc.vector.scalar_tensor_tensor(
                    out=lead[:], in0=stage[f][:], scalar=quad_cols[:, s, f, o : o + 1],
                    in1=lead[:], op0=ALU.add, op1=ALU.max,
                )

            def finish():
                if o == 0:
                    y = quad_results.tile([P, PART_BLOCKS, 2, HEADS, DK], F32)
                    stage["y"] = y
                quad_max = banks.tile([P, PART_BLOCKS, P], F32, tag="bank")
                for b in range(PART_BLOCKS):
                    cols = slice(b * P, (b + 1) * P)
                    nc.tensor.matmul(
                        out=quad_max[:, b, :], lhsT=tiles["first"][:, cols], rhs=ident[:],
                        start=True, stop=False, is_transpose=True,
                    )
                    nc.tensor.matmul(
                        out=quad_max[:, b, :], lhsT=tiles["lead"][:, cols], rhs=ident[:],
                        start=False, stop=True, is_transpose=True,
                    )
                nc.vector.tensor_reduce(
                    out=stage["y"][:].rearrange("p b g h o -> p b (g h) o")[:, :, :, o],
                    in_=quad_max[:].rearrange("p b (c i) -> p b c i", i=QUARTER),
                    axis=X_AXIS,
                    op=ALU.max,
                )

            return [feed, lambda: grow(2), lambda: grow(3), finish]

        def quad_store(s, stage):
            for b in range(PART_BLOCKS):
                for g in range(2):
                    j = 2 if s == 1 else g
                    part = QUAD_PARTS[s][g if s == 1 else 0]
                    store_block(j, part * PART + b * P, stage["y"][:, b, g, :, :])

        def quad_run(s, stage, keep, first_bank):
            work = [(first_bank, keep)]
            for o in range(DK):
                at = first_bank + o * QUAD_EVERY
                feed, grow_2, grow_3, finish = quad_unit(s, stage, o)
                work += [(at - 4, feed), (at + 3, grow_2), (at + 6, grow_3), (at + 13, finish)]
            work += [(first_bank + DK * QUAD_EVERY + 5, lambda: quad_store(s, stage))]
            for bank, piece in work:
                events.setdefault(bank, []).append(piece)
            return first_bank + (DK - 1) * QUAD_EVERY + 6

        def together(*steps):
            def run():
                for step in steps:
                    step()
            return run

        def spread(steps, every):
            spaced = []
            for step in steps:
                spaced += [step] + pause(every - 1)
            return spaced

        def warm_up():
            mx_pass(0, w_codes[:, 0, 0, :], w_scales[:, 0, 0, :])

        todo = []
        taken = [0]

        def advance():
            if taken[0] < len(todo):
                todo[taken[0]]()
                taken[0] += 1

        def finish_steps():
            while taken[0] < len(todo):
                advance()

        def sweep(g_lo, g_step, j, o_range, y, blocks):
            for o in o_range:
                tropical(g_lo, g_step, j, o, y, blocks)
                advance()

        head_parts = 2
        edge = DK // 4
        last_edge = DK // 8
        last_growth = [0]

        def start_quads(s, stage, keep):
            first_bank = max(banks_done[0] + 5, last_growth[0] + 7)
            last_growth[0] = quad_run(s, stage, keep, first_bank)

        def prepare_quads(s, between):
            logs_first, turns, keep, stage = quad_steps(s)
            return logs_first, between + turns + [lambda: start_quads(s, stage, keep)]

        j, parts = STAGES[0]
        g_lo, g_step, log_parts = log_steps(j, parts, first=True)
        for step in log_parts[: 2 * head_parts]:
            step()
        with tc.manual_schedule(engines={mybir.EngineType.DVE, mybir.EngineType.PE}):
            a0, a1, a2 = x_steps(2)
            b0, b1, b2 = x_steps(3)
            todo.extend([together(a0, warm_up), together(a1, warm_up), together(b0, warm_up)])
            todo.extend([together(b1, warm_up, a2), pause(1)[0]])
            todo.extend(log_parts[4:6] + [b2] + pause(1) + log_parts[6:])
            for stage, (j, parts) in enumerate(STAGES):
                blocks = range(len(parts) * PART_BLOCKS)
                halves = [range(0, len(blocks) // 2), range(len(blocks) // 2, len(blocks))]
                y = results.tile([P, len(blocks), HEADS, DK], F32)
                start_o = 0
                if stage == 0:
                    sweep(g_lo, g_step, j, range(edge), y, halves[0])
                    finish_steps()
                    start_o = edge
                    for f in range(4):
                        quad_weights(0, f)
                if stage + 1 < len(STAGES):
                    next_lo, next_step, log_parts = log_steps(*STAGES[stage + 1])
                if stage == 0:
                    constants = [lambda g=g: quad_constants(g) for g in range(2)]
                    constants += [lambda s=s: quad_turn_constants(s) for s in range(2)]
                    quad_logs, quad_rest = prepare_quads(0, constants + pause(2))
                    a0, a1, a2 = x_steps(7)
                    todo.extend([together(a0, log_parts[0]), together(a1, log_parts[1])])
                    todo.extend(pause(1) + [together(log_parts[2], a2)] + pause(1))
                    todo.extend(quad_logs + quad_rest + spread(log_parts[3:], 6))
                elif stage == 1:
                    quad_logs, quad_rest = prepare_quads(1, pause(4))
                    a0, a1, a2 = x_steps(6)
                    b0, b1, b2 = x_steps(4)
                    c0, c1, c2 = x_steps(5)
                    todo.extend(spread([
                        together(a0, log_parts[0]),
                        together(a1, log_parts[1]),
                        together(b0, log_parts[2], a2),
                        together(b1, log_parts[3]),
                        together(c0, log_parts[4], b2),
                        together(c1, log_parts[5]),
                        together(log_parts[6], c2),
                        log_parts[7],
                    ], 5))
                    todo.extend([lambda f=f: quad_weights(1, f) for f in range(4)])
                    todo.extend(spread(quad_logs, 2))
                elif stage == 2:
                    todo.extend(quad_rest + spread(log_parts, 7))
                elif stage + 1 < len(STAGES):
                    todo.extend(spread(log_parts, 8))
                else:
                    todo.extend(pause(4) + spread([warm_up] * 6, 8))
                if stage == 0:
                    sweep(g_lo, g_step, j, range(edge), y, halves[1])
                if stage + 1 < len(STAGES):
                    sweep(g_lo, g_step, j, range(start_o, DK), y, blocks)
                    finish_steps()
                    store(j, parts, y, blocks)
                    g_lo, g_step = next_lo, next_step
                else:
                    sweep(g_lo, g_step, j, range(start_o, DK - last_edge), y, blocks)
                    for half in halves:
                        sweep(g_lo, g_step, j, range(DK - last_edge, DK), y, half)
                        store(j, parts, y, half)
